import numpy as np
import ml_dtypes


def mxq(x, axis, fmt="e4m3"):
    dtype, down = {"e4m3": (ml_dtypes.float8_e4m3fn, 7), "e5m2": (ml_dtypes.float8_e5m2, 14)}[fmt]
    v = np.moveaxis(np.asarray(x, np.float32).astype(ml_dtypes.bfloat16).astype(np.float64), axis, -1)
    blocks = v.reshape(v.shape[:-1] + (-1, 32))
    amax = np.abs(blocks).max(-1, keepdims=True)
    byte = np.maximum(np.where(amax > 0, np.frexp(amax)[1] - 1 + 127, 0) - down, 1)
    scale = np.exp2(byte - 127.0)
    codes = (blocks / scale).astype(np.float32).astype(dtype).astype(np.float64)
    return np.moveaxis((codes * scale).reshape(v.shape), -1, axis)


WIDE = False


def mx_kscale(k):
    if not WIDE:
        return np.ones(k)
    levels = np.array([10, -10, 5, -5, 0])
    a = np.random.permutation(np.resize(levels, k // 512 * 4)).reshape(k // 512, 4)
    idx = np.arange(k)
    return np.exp2(a[idx // 512, idx % 128 // 32])


BF16 = ml_dtypes.bfloat16


def bf(x):
    return np.asarray(x, np.float32).astype(BF16)


def f64(x):
    return np.asarray(x).astype(np.float64)


B, N = 2048, 1024
SLOPE = 0.01


def setup_inputs():
    s = mx_kscale(B)
    level = np.random.standard_normal(N) * 2.5 - 1.5
    return {"potential": bf((np.random.standard_normal((B, N)) * 2.2 + level) * s[:, None]),
            "contribution": bf(np.random.random(B) / (s * s))}


def reference(potential, contribution):
    p = f64(potential)
    activation = np.where(p >= 0, p, SLOPE * p)
    weighted = activation * f64(contribution)[:, None]
    return (mxq(weighted, 0, "e4m3").T @ mxq(activation, 0, "e4m3")) / B

@@ -1,0 +1,153 @@
+from contextlib import ExitStack
+
+import concourse.bass as bass
+import concourse.mybir as mybir
+import concourse.tile as tile
+
+F32 = mybir.dt.float32
+BF16 = mybir.dt.bfloat16
+U32 = mybir.dt.uint32
+U8 = mybir.dt.uint8
+FP8X4 = mybir.dt.float8_e4m3fn_x4
+ALU = mybir.AluOpType
+ACT = mybir.ActivationFunctionType
+
+P = 128
+B = 2048
+N = 1024
+PACK = 4
+PASSES = B // (P * PACK)
+ROWS = PASSES * PACK
+BLK = 256
+NBLK = N // BLK
+SLOPE = 0.01
+FLOPS = 2 * B * N * N
+
+AR_ON_VECTOR = (3,)
+WR_ON_VECTOR = (3,)
+
+
+def tile_mnelayer_pb_kernel(tc, potential, contribution, out):
+    nc = tc.nc
+    pot = potential.rearrange("(c p j) w -> c p j w", c=PASSES, p=P, j=PACK)
+    out_v = out.rearrange("(u m p) n -> u p m n", m=2, p=P)
+
+    with ExitStack() as ctx:
+        keep = ctx.enter_context(tc.tile_pool(name="keep", bufs=1))
+        work = ctx.enter_context(tc.tile_pool(name="work", bufs=2))
+        stage = ctx.enter_context(tc.tile_pool(name="stage", bufs=4))
+        psum = ctx.enter_context(tc.psum_pool(name="psum", bufs=6))
+        ctx.enter_context(tc.manual_schedule())
+
+        c_bf = keep.tile([P, ROWS], BF16, name="c_bf")
+        c_32 = keep.tile([P, ROWS], F32, name="c_32")
+        p_first = keep.tile([P, ROWS, BLK], BF16, name="p_first")
+        p_rest = keep.tile([P, ROWS, N - BLK], BF16, name="p_rest")
+        a_codes = [keep.tile([P, PASSES, BLK], U32, name="a_codes%d" % b, align_bytes=64) for b in range(NBLK)]
+        a_scales = [keep.tile([P, PASSES, BLK], U8, name="a_scales%d" % b, align_bytes=64) for b in range(NBLK)]
+        w_codes = [keep.tile([P, PASSES, BLK], U32, name="w_codes%d" % b, align_bytes=64) for b in range(NBLK)]
+        w_scales = [keep.tile([P, PASSES, BLK], U8, name="w_scales%d" % b, align_bytes=64) for b in range(NBLK)]
+
+        nc.scalar.dma_start(
+            out=c_bf[:].rearrange("p (c j) -> p c j", j=PACK),
+            in_=contribution.rearrange("(c p j) -> p c j", c=PASSES, p=P),
+        )
+        for c in range(PASSES):
+            nc.sync.dma_start(out=p_first[:, PACK * c : PACK * (c + 1), :], in_=pot[c][:, :, 0:BLK])
+        for c in range(PASSES):
+            nc.sync.dma_start(out=p_rest[:, PACK * c : PACK * (c + 1), :], in_=pot[c][:, :, BLK:N])
+
+        leaky = {}
+        weighted = {}
+        a_grp = {}
+        w_grp = {}
+
+        def p_rows(b, c):
+            rows = slice(PACK * c, PACK * (c + 1))
+            if b == 0:
+                return p_first[:, rows, :]
+            return p_rest[:, rows, BLK * (b - 1) : BLK * b]
+
+        def leaky_relu(b, c):
+            src = p_rows(b, c)
+            nc.vector.scalar_tensor_tensor(
+                out=leaky[b][:, PACK * c : PACK * (c + 1), :],
+                in0=src, scalar=SLOPE, in1=src, op0=ALU.mult, op1=ALU.max,
+            )
+
+        def regroup(on_vector, dst, src, c):
+            o = dst[:, c].rearrange("p (g i) j -> p g j i", i=4)
+            s = src[:, PACK * c : PACK * (c + 1), :].rearrange("p j (g i) -> p g j i", i=4)
+            if on_vector:
+                nc.vector.tensor_copy(out=o, in_=s)
+            else:
+                nc.scalar.copy(out=o, in_=s)
+
+        def quantise(grp, codes, scales):
+            nc.vector.quantize_mx(
+                out=codes[:].rearrange("p c w -> p (c w)").bitcast(FP8X4),
+                scales=scales[:].rearrange("p c w -> p (c w)"),
+                in_=grp[:].rearrange("p c w j -> p (c w j)"),
+            )
+
+        banks = {}
+
+        def multiply(u, b):
+            acc = psum.tile([P, 2, BLK], F32, name="acc")
+            banks[(u, b)] = acc
+            for m in range(2):
+                for c in range(PASSES):
+                    nc.tensor.matmul_mx(
+                        out=acc[:, m, :],
+                        lhsT=w_codes[u][:, c, P * m : P * (m + 1)].bitcast(FP8X4),
+                        lhsT_scale=w_scales[u][:, c, P * m : P * (m + 1)],
+                        rhs=a_codes[b][:, c, :].bitcast(FP8X4),
+                        rhs_scale=a_scales[b][:, c, :],
+                        start=(c == 0),
+                        stop=(c == PASSES - 1),
+                    )
+
+        def finish(u, b):
+            res = stage.tile([P, 2, BLK], F32, name="res")
+            nc.scalar.activation(out=res[:], in_=banks[(u, b)][:], func=ACT.Copy, scale=1.0 / B)
+            nc.sync.dma_start(out=out_v[u][:, :, BLK * b : BLK * (b + 1)], in_=res[:])
+
+        for b in range(NBLK):
+            leaky[b] = work.tile([P, ROWS, BLK], F32, name="leaky")
+            weighted[b] = work.tile([P, ROWS, BLK], BF16, name="weighted")
+            a_grp[b] = work.tile([P, PASSES, BLK, PACK], BF16, name="a_grp", align_bytes=64)
+            w_grp[b] = work.tile([P, PASSES, BLK, PACK], BF16, name="w_grp", align_bytes=64)
+
+            leaky_relu(b, 0)
+            leaky_relu(b, 1)
+            if b == 0:
+                nc.vector.tensor_copy(out=c_32[:], in_=c_bf[:])
+            else:
+                quantise(w_grp[b - 1], w_codes[b - 1], w_scales[b - 1])
+                for bb in range(b):
+                    multiply(b - 1, bb)
+            leaky_relu(b, 2)
+            leaky_relu(b, 3)
+            for c in range(PASSES):
+                regroup(c in AR_ON_VECTOR, a_grp[b], leaky[b], c)
+            for r in range(ROWS):
+                nc.vector.tensor_scalar(
+                    out=weighted[b][:, r, :], in0=leaky[b][:, r, :],
+                    scalar1=c_32[:, r : r + 1], scalar2=None, op0=ALU.mult,
+                )
+            quantise(a_grp[b], a_codes[b], a_scales[b])
+            if b > 0:
+                for bb in range(b):
+                    finish(b - 1, bb)
+            for u in range(b):
+                multiply(u, b)
+            for c in range(PASSES):
+                regroup(c in WR_ON_VECTOR, w_grp[b], weighted[b], c)
+            for u in range(b):
+                finish(u, b)
+
+        last = NBLK - 1
+        quantise(w_grp[last], w_codes[last], w_scales[last])
+        for bb in range(NBLK):
+            multiply(last, bb)
+            finish(last, bb)

@@ -1,8 +1,6 @@
 from contextlib import ExitStack
 
-import concourse.bass as bass
 import concourse.mybir as mybir
-import concourse.tile as tile
 
 F32 = mybir.dt.float32
 BF16 = mybir.dt.bfloat16
@@ -20,33 +18,40 @@ PASSES = B // (P * PACK)
 ROWS = PASSES * PACK
 BLK = 256
 NBLK = N // BLK
+UNITS = NBLK * PASSES
+HALF = 512
 SLOPE = 0.01
 FLOPS = 2 * B * N * N
 
-AR_ON_VECTOR = (3,)
-WR_ON_VECTOR = (3,)
+A_LAG = 2
+W_LAG = 2
+AR_ON_VECTOR = ()
+WR_ON_VECTOR = (3, 7, 11, 15)
+OUT_ON_VECTOR = ((0, 3), (1, 3), (2, 3), (3, 1), (3, 3))
+OUT_DELAY = 1
+OUT_PER_STEP = 2
 
 
 def tile_mnelayer_pb_kernel(tc, potential, contribution, out):
     nc = tc.nc
     pot = potential.rearrange("(c p j) w -> c p j w", c=PASSES, p=P, j=PACK)
-    out_v = out.rearrange("(u m p) n -> u p m n", m=2, p=P)
 
     with ExitStack() as ctx:
         keep = ctx.enter_context(tc.tile_pool(name="keep", bufs=1))
-        work = ctx.enter_context(tc.tile_pool(name="work", bufs=2))
-        stage = ctx.enter_context(tc.tile_pool(name="stage", bufs=4))
-        psum = ctx.enter_context(tc.psum_pool(name="psum", bufs=6))
+        work = ctx.enter_context(tc.tile_pool(name="work", bufs=4))
+        stage = ctx.enter_context(tc.tile_pool(name="stage", bufs=6))
+        psum = ctx.enter_context(tc.psum_pool(name="psum", bufs=8))
         ctx.enter_context(tc.manual_schedule())
 
         c_bf = keep.tile([P, ROWS], BF16, name="c_bf")
         c_32 = keep.tile([P, ROWS], F32, name="c_32")
         p_first = keep.tile([P, ROWS, BLK], BF16, name="p_first")
         p_rest = keep.tile([P, ROWS, N - BLK], BF16, name="p_rest")
-        a_codes = [keep.tile([P, PASSES, BLK], U32, name="a_codes%d" % b, align_bytes=64) for b in range(NBLK)]
-        a_scales = [keep.tile([P, PASSES, BLK], U8, name="a_scales%d" % b, align_bytes=64) for b in range(NBLK)]
-        w_codes = [keep.tile([P, PASSES, BLK], U32, name="w_codes%d" % b, align_bytes=64) for b in range(NBLK)]
-        w_scales = [keep.tile([P, PASSES, BLK], U8, name="w_scales%d" % b, align_bytes=64) for b in range(NBLK)]
+        leaky = [keep.tile([P, ROWS, BLK], F32, name="leaky%d" % b) for b in range(NBLK)]
+        a_codes = keep.tile([P, PASSES, N], U32, name="a_codes", align_bytes=64)
+        a_scales = keep.tile([P, PASSES, N], U8, name="a_scales", align_bytes=64)
+        w_codes = keep.tile([P, PASSES, N], U32, name="w_codes", align_bytes=64)
+        w_scales = keep.tile([P, PASSES, N], U8, name="w_scales", align_bytes=64)
 
         nc.scalar.dma_start(
             out=c_bf[:].rearrange("p (c j) -> p c j", j=PACK),
@@ -57,97 +62,110 @@ def tile_mnelayer_pb_kernel(tc, potential, contribution, out):
         for c in range(PASSES):
             nc.sync.dma_start(out=p_rest[:, PACK * c : PACK * (c + 1), :], in_=pot[c][:, :, BLK:N])
 
-        leaky = {}
-        weighted = {}
-        a_grp = {}
-        w_grp = {}
+        def rows_of(c):
+            return slice(PACK * c, PACK * (c + 1))
 
-        def p_rows(b, c):
-            rows = slice(PACK * c, PACK * (c + 1))
+        def leaky_relu(i):
+            b, c = divmod(i, PASSES)
             if b == 0:
-                return p_first[:, rows, :]
-            return p_rest[:, rows, BLK * (b - 1) : BLK * b]
-
-        def leaky_relu(b, c):
-            src = p_rows(b, c)
+                src = p_first[:, rows_of(c), :]
+            else:
+                src = p_rest[:, rows_of(c), BLK * (b - 1) : BLK * b]
             nc.vector.scalar_tensor_tensor(
-                out=leaky[b][:, PACK * c : PACK * (c + 1), :],
-                in0=src, scalar=SLOPE, in1=src, op0=ALU.mult, op1=ALU.max,
+                out=leaky[b][:, rows_of(c), :], in0=src, scalar=SLOPE, in1=src, op0=ALU.mult, op1=ALU.max,
             )
 
-        def regroup(on_vector, dst, src, c):
-            o = dst[:, c].rearrange("p (g i) j -> p g j i", i=4)
-            s = src[:, PACK * c : PACK * (c + 1), :].rearrange("p j (g i) -> p g j i", i=4)
+        def regroup(on_vector, dst, src):
+            o = dst[:].rearrange("p (g i) j -> p g j i", i=4)
+            s = src.rearrange("p j (g i) -> p g j i", i=4)
             if on_vector:
                 nc.vector.tensor_copy(out=o, in_=s)
             else:
                 nc.scalar.copy(out=o, in_=s)
 
-        def quantise(grp, codes, scales):
+        def quantise(i, grp, codes, scales):
+            b, c = divmod(i, PASSES)
+            cols = slice(BLK * b, BLK * (b + 1))
             nc.vector.quantize_mx(
-                out=codes[:].rearrange("p c w -> p (c w)").bitcast(FP8X4),
-                scales=scales[:].rearrange("p c w -> p (c w)"),
-                in_=grp[:].rearrange("p c w j -> p (c w j)"),
+                out=codes[:, c, cols].bitcast(FP8X4),
+                scales=scales[:, c, cols],
+                in_=grp[:].rearrange("p w j -> p (w j)"),
             )
 
-        banks = {}
+        a_grp = {}
+        w_grp = {}
+        acc = {}
+        waiting = []
 
-        def multiply(u, b):
-            acc = psum.tile([P, 2, BLK], F32, name="acc")
-            banks[(u, b)] = acc
+        def activation_unit(i):
+            b, c = divmod(i, PASSES)
+            a_grp[i] = work.tile([P, BLK, PACK], BF16, name="a_grp", align_bytes=64)
+            regroup(i in AR_ON_VECTOR, a_grp[i], leaky[b][:, rows_of(c), :])
+
+        def weighted_unit(i):
+            u, c = divmod(i, PASSES)
+            weighted = work.tile([P, PACK, BLK], BF16, name="weighted")
+            for j in range(PACK):
+                r = PACK * c + j
+                nc.vector.tensor_scalar(
+                    out=weighted[:, j, :], in0=leaky[u][:, r, :],
+                    scalar1=c_32[:, r : r + 1], scalar2=None, op0=ALU.mult,
+                )
+            return weighted
+
+        def multiply(i, step):
+            u, c = divmod(i, PASSES)
+            quantise(i, w_grp[i], w_codes, w_scales)
             for m in range(2):
-                for c in range(PASSES):
+                for h in range(2):
+                    if c == 0:
+                        acc[(u, m, h)] = psum.tile([P, HALF], F32, name="acc")
+                    lcols = slice(BLK * u + P * m, BLK * u + P * (m + 1))
+                    rcols = slice(HALF * h, HALF * (h + 1))
                     nc.tensor.matmul_mx(
-                        out=acc[:, m, :],
-                        lhsT=w_codes[u][:, c, P * m : P * (m + 1)].bitcast(FP8X4),
-                        lhsT_scale=w_scales[u][:, c, P * m : P * (m + 1)],
-                        rhs=a_codes[b][:, c, :].bitcast(FP8X4),
-                        rhs_scale=a_scales[b][:, c, :],
+                        out=acc[(u, m, h)][:],
+                        lhsT=w_codes[:, c, lcols].bitcast(FP8X4),
+                        lhsT_scale=w_scales[:, c, lcols],
+                        rhs=a_codes[:, c, rcols].bitcast(FP8X4),
+                        rhs_scale=a_scales[:, c, rcols],
                         start=(c == 0),
                         stop=(c == PASSES - 1),
                     )
+                    if c == PASSES - 1:
+                        waiting.append((step, u, m, h))
 
-        def finish(u, b):
-            res = stage.tile([P, 2, BLK], F32, name="res")
-            nc.scalar.activation(out=res[:], in_=banks[(u, b)][:], func=ACT.Copy, scale=1.0 / B)
-            nc.sync.dma_start(out=out_v[u][:, :, BLK * b : BLK * (b + 1)], in_=res[:])
-
-        for b in range(NBLK):
-            leaky[b] = work.tile([P, ROWS, BLK], F32, name="leaky")
-            weighted[b] = work.tile([P, ROWS, BLK], BF16, name="weighted")
-            a_grp[b] = work.tile([P, PASSES, BLK, PACK], BF16, name="a_grp", align_bytes=64)
-            w_grp[b] = work.tile([P, PASSES, BLK, PACK], BF16, name="w_grp", align_bytes=64)
-
-            leaky_relu(b, 0)
-            leaky_relu(b, 1)
-            if b == 0:
-                nc.vector.tensor_copy(out=c_32[:], in_=c_bf[:])
+        def finish(u, m, h):
+            res = stage.tile([P, HALF], F32, name="res")
+            if (u, 2 * m + h) in OUT_ON_VECTOR:
+                nc.vector.tensor_scalar(out=res[:], in0=acc[(u, m, h)][:], scalar1=1.0 / B, scalar2=None, op0=ALU.mult)
             else:
-                quantise(w_grp[b - 1], w_codes[b - 1], w_scales[b - 1])
-                for bb in range(b):
-                    multiply(b - 1, bb)
-            leaky_relu(b, 2)
-            leaky_relu(b, 3)
-            for c in range(PASSES):
-                regroup(c in AR_ON_VECTOR, a_grp[b], leaky[b], c)
-            for r in range(ROWS):
-                nc.vector.tensor_scalar(
-                    out=weighted[b][:, r, :], in0=leaky[b][:, r, :],
-                    scalar1=c_32[:, r : r + 1], scalar2=None, op0=ALU.mult,
-                )
-            quantise(a_grp[b], a_codes[b], a_scales[b])
-            if b > 0:
-                for bb in range(b):
-                    finish(b - 1, bb)
-            for u in range(b):
-                multiply(u, b)
-            for c in range(PASSES):
-                regroup(c in WR_ON_VECTOR, w_grp[b], weighted[b], c)
-            for u in range(b):
-                finish(u, b)
+                nc.scalar.activation(out=res[:], in_=acc[(u, m, h)][:], func=ACT.Copy, scale=1.0 / B)
+            row0 = BLK * u + P * m
+            nc.sync.dma_start(out=out[row0 : row0 + P, HALF * h : HALF * (h + 1)], in_=res[:])
 
-        last = NBLK - 1
-        quantise(w_grp[last], w_codes[last], w_scales[last])
-        for bb in range(NBLK):
-            multiply(last, bb)
-            finish(last, bb)
+        for i in range(UNITS):
+            leaky_relu(i)
+            if i == 1:
+                nc.vector.tensor_copy(out=c_32[:], in_=c_bf[:])
+            activation_unit(i)
+            if i >= A_LAG:
+                quantise(i - A_LAG, a_grp[i - A_LAG], a_codes, a_scales)
+
+        late = list(range(UNITS - A_LAG, UNITS))
+        for i in range(UNITS):
+            weighted = weighted_unit(i)
+            if late:
+                k = late.pop(0)
+                quantise(k, a_grp[k], a_codes, a_scales)
+            w_grp[i] = work.tile([P, BLK, PACK], BF16, name="w_grp", align_bytes=64)
+            regroup(i in WR_ON_VECTOR, w_grp[i], weighted[:])
+            if i >= W_LAG:
+                multiply(i - W_LAG, i)
+            done = 0
+            while waiting and waiting[0][0] <= i - OUT_DELAY and done < OUT_PER_STEP:
+                finish(*waiting.pop(0)[1:])
+                done += 1
+        for i in range(UNITS - W_LAG, UNITS):
+            multiply(i, UNITS)
+        while waiting:
+            finish(*waiting.pop(0)[1:])

@@ -30,6 +30,7 @@ WR_ON_VECTOR = (3, 7, 11, 15)
 OUT_ON_VECTOR = ((0, 3), (1, 3), (2, 3), (3, 1), (3, 3))
 OUT_DELAY = 1
 OUT_PER_STEP = 2
+WARM_PASSES = 3
 
 
 def tile_mnelayer_pb_kernel(tc, potential, contribution, out):
@@ -143,6 +144,20 @@ def tile_mnelayer_pb_kernel(tc, potential, contribution, out):
             row0 = BLK * u + P * m
             nc.sync.dma_start(out=out[row0 : row0 + P, HALF * h : HALF * (h + 1)], in_=res[:])
 
+        warm_bank = psum.tile([P, HALF], F32, name="acc")
+
+        def warm_up(c):
+            for n in range(WARM_PASSES):
+                nc.tensor.matmul_mx(
+                    out=warm_bank[:],
+                    lhsT=a_codes[:, c, N - P : N].bitcast(FP8X4),
+                    lhsT_scale=a_scales[:, c, N - P : N],
+                    rhs=a_codes[:, c, HALF:N].bitcast(FP8X4),
+                    rhs_scale=a_scales[:, c, HALF:N],
+                    start=True,
+                    stop=True,
+                )
+
         for i in range(UNITS):
             leaky_relu(i)
             if i == 1:
@@ -150,6 +165,8 @@ def tile_mnelayer_pb_kernel(tc, potential, contribution, out):
             activation_unit(i)
             if i >= A_LAG:
                 quantise(i - A_LAG, a_grp[i - A_LAG], a_codes, a_scales)
+                if i - A_LAG >= UNITS - PASSES:
+                    warm_up(i - A_LAG - (UNITS - PASSES))
 
         late = list(range(UNITS - A_LAG, UNITS))
         for i in range(UNITS):
@@ -157,6 +174,8 @@ def tile_mnelayer_pb_kernel(tc, potential, contribution, out):
             if late:
                 k = late.pop(0)
                 quantise(k, a_grp[k], a_codes, a_scales)
+                if k < UNITS - 1:
+                    warm_up(k - (UNITS - PASSES))
             w_grp[i] = work.tile([P, BLK, PACK], BF16, name="w_grp", align_bytes=64)
             regroup(i in WR_ON_VECTOR, w_grp[i], weighted[:])
             if i >= W_LAG:

@@ -17,20 +17,19 @@ PACK = 4
 PASSES = B // (P * PACK)
 ROWS = PASSES * PACK
 BLK = 256
-NBLK = N // BLK
-UNITS = NBLK * PASSES
 HALF = 512
+A_UNITS = PASSES * (N // HALF)
+W_UNITS = (N // BLK) * PASSES
 SLOPE = 0.01
 FLOPS = 2 * B * N * N
 
 A_LAG = 2
 W_LAG = 2
-AR_ON_VECTOR = ()
-WR_ON_VECTOR = (3, 7, 11, 15)
+FIRST_W = 4
+WR_ON_VECTOR = (3, 7, 11)
 OUT_ON_VECTOR = ((0, 3), (1, 3), (2, 3), (3, 1), (3, 3))
-OUT_DELAY = 1
+OUT_DELAY = 2
 OUT_PER_STEP = 2
-WARM_PASSES = 3
 
 
 def tile_mnelayer_pb_kernel(tc, potential, contribution, out):
@@ -39,16 +38,15 @@ def tile_mnelayer_pb_kernel(tc, potential, contribution, out):
 
     with ExitStack() as ctx:
         keep = ctx.enter_context(tc.tile_pool(name="keep", bufs=1))
-        work = ctx.enter_context(tc.tile_pool(name="work", bufs=4))
-        stage = ctx.enter_context(tc.tile_pool(name="stage", bufs=6))
+        wide = ctx.enter_context(tc.tile_pool(name="wide", bufs=4))
+        work = ctx.enter_context(tc.tile_pool(name="work", bufs=6))
         psum = ctx.enter_context(tc.psum_pool(name="psum", bufs=8))
         ctx.enter_context(tc.manual_schedule())
 
         c_bf = keep.tile([P, ROWS], BF16, name="c_bf")
         c_32 = keep.tile([P, ROWS], F32, name="c_32")
-        p_first = keep.tile([P, ROWS, BLK], BF16, name="p_first")
-        p_rest = keep.tile([P, ROWS, N - BLK], BF16, name="p_rest")
-        leaky = [keep.tile([P, ROWS, BLK], F32, name="leaky%d" % b) for b in range(NBLK)]
+        p_in = [keep.tile([P, PACK, N], BF16, name="p_in%d" % c) for c in range(PASSES)]
+        leaky = [keep.tile([P, PACK, N], F32, name="leaky%d" % c) for c in range(PASSES)]
         a_codes = keep.tile([P, PASSES, N], U32, name="a_codes", align_bytes=64)
         a_scales = keep.tile([P, PASSES, N], U8, name="a_scales", align_bytes=64)
         w_codes = keep.tile([P, PASSES, N], U32, name="w_codes", align_bytes=64)
@@ -58,22 +56,16 @@ def tile_mnelayer_pb_kernel(tc, potential, contribution, out):
             out=c_bf[:].rearrange("p (c j) -> p c j", j=PACK),
             in_=contribution.rearrange("(c p j) -> p c j", c=PASSES, p=P),
         )
-        for c in range(PASSES):
-            nc.sync.dma_start(out=p_first[:, PACK * c : PACK * (c + 1), :], in_=pot[c][:, :, 0:BLK])
-        for c in range(PASSES):
-            nc.sync.dma_start(out=p_rest[:, PACK * c : PACK * (c + 1), :], in_=pot[c][:, :, BLK:N])
+        for q in range(N // BLK):
+            cols = slice(BLK * q, BLK * (q + 1))
+            nc.sync.dma_start(out=p_in[0][:, :, cols], in_=pot[0][:, :, cols])
+        for c in range(1, PASSES):
+            nc.sync.dma_start(out=p_in[c][:], in_=pot[c])
 
-        def rows_of(c):
-            return slice(PACK * c, PACK * (c + 1))
-
-        def leaky_relu(i):
-            b, c = divmod(i, PASSES)
-            if b == 0:
-                src = p_first[:, rows_of(c), :]
-            else:
-                src = p_rest[:, rows_of(c), BLK * (b - 1) : BLK * b]
+        def leaky_relu(c, cols):
             nc.vector.scalar_tensor_tensor(
-                out=leaky[b][:, rows_of(c), :], in0=src, scalar=SLOPE, in1=src, op0=ALU.mult, op1=ALU.max,
+                out=leaky[c][:, :, cols], in0=p_in[c][:, :, cols], scalar=SLOPE, in1=p_in[c][:, :, cols],
+                op0=ALU.mult, op1=ALU.max,
             )
 
         def regroup(on_vector, dst, src):
@@ -84,9 +76,7 @@ def tile_mnelayer_pb_kernel(tc, potential, contribution, out):
             else:
                 nc.scalar.copy(out=o, in_=s)
 
-        def quantise(i, grp, codes, scales):
-            b, c = divmod(i, PASSES)
-            cols = slice(BLK * b, BLK * (b + 1))
+        def quantise(grp, codes, scales, c, cols):
             nc.vector.quantize_mx(
                 out=codes[:, c, cols].bitcast(FP8X4),
                 scales=scales[:, c, cols],
@@ -97,26 +87,43 @@ def tile_mnelayer_pb_kernel(tc, potential, contribution, out):
         w_grp = {}
         acc = {}
         waiting = []
+        count = {"a_done": 0, "w_next": 0, "w_done": 0, "step": 0}
 
         def activation_unit(i):
-            b, c = divmod(i, PASSES)
-            a_grp[i] = work.tile([P, BLK, PACK], BF16, name="a_grp", align_bytes=64)
-            regroup(i in AR_ON_VECTOR, a_grp[i], leaky[b][:, rows_of(c), :])
+            c, h = divmod(i, 2)
+            if c == 0:
+                for q in range(2):
+                    leaky_relu(c, slice(HALF * h + BLK * q, HALF * h + BLK * (q + 1)))
+            else:
+                leaky_relu(c, slice(HALF * h, HALF * (h + 1)))
+            a_grp[i] = wide.tile([P, HALF, PACK], BF16, name="a_grp", align_bytes=64)
+            regroup(False, a_grp[i], leaky[c][:, :, HALF * h : HALF * (h + 1)])
 
-        def weighted_unit(i):
-            u, c = divmod(i, PASSES)
+        def quantise_activation():
+            i = count["a_done"]
+            c, h = divmod(i, 2)
+            quantise(a_grp[i], a_codes, a_scales, c, slice(HALF * h, HALF * (h + 1)))
+            count["a_done"] = i + 1
+
+        def scale_rows(k):
+            u, c = divmod(k, PASSES)
             weighted = work.tile([P, PACK, BLK], BF16, name="weighted")
             for j in range(PACK):
                 r = PACK * c + j
                 nc.vector.tensor_scalar(
-                    out=weighted[:, j, :], in0=leaky[u][:, r, :],
+                    out=weighted[:, j, :], in0=leaky[c][:, j, BLK * u : BLK * (u + 1)],
                     scalar1=c_32[:, r : r + 1], scalar2=None, op0=ALU.mult,
                 )
             return weighted
 
-        def multiply(i, step):
-            u, c = divmod(i, PASSES)
-            quantise(i, w_grp[i], w_codes, w_scales)
+        def regroup_weighted(k, weighted):
+            w_grp[k] = work.tile([P, BLK, PACK], BF16, name="w_grp", align_bytes=64)
+            regroup(k in WR_ON_VECTOR, w_grp[k], weighted[:])
+            count["w_next"] = k + 1
+
+        def multiply(k):
+            u, c = divmod(k, PASSES)
+            quantise(w_grp[k], w_codes, w_scales, c, slice(BLK * u, BLK * (u + 1)))
             for m in range(2):
                 for h in range(2):
                     if c == 0:
@@ -133,10 +140,16 @@ def tile_mnelayer_pb_kernel(tc, potential, contribution, out):
                         stop=(c == PASSES - 1),
                     )
                     if c == PASSES - 1:
-                        waiting.append((step, u, m, h))
+                        waiting.append((count["step"], u, m, h))
+            count["w_done"] = k + 1
+
+        def multiply_if_ready():
+            k = count["w_done"]
+            if count["w_next"] - k > W_LAG and count["a_done"] >= 2 * (k % PASSES) + 2:
+                multiply(k)
 
         def finish(u, m, h):
-            res = stage.tile([P, HALF], F32, name="res")
+            res = work.tile([P, HALF], F32, name="res")
             if (u, 2 * m + h) in OUT_ON_VECTOR:
                 nc.vector.tensor_scalar(out=res[:], in0=acc[(u, m, h)][:], scalar1=1.0 / B, scalar2=None, op0=ALU.mult)
             else:
@@ -144,47 +157,31 @@ def tile_mnelayer_pb_kernel(tc, potential, contribution, out):
             row0 = BLK * u + P * m
             nc.sync.dma_start(out=out[row0 : row0 + P, HALF * h : HALF * (h + 1)], in_=res[:])
 
-        warm_bank = psum.tile([P, HALF], F32, name="acc")
-
-        def warm_up(c):
-            for n in range(WARM_PASSES):
-                nc.tensor.matmul_mx(
-                    out=warm_bank[:],
-                    lhsT=a_codes[:, c, N - P : N].bitcast(FP8X4),
-                    lhsT_scale=a_scales[:, c, N - P : N],
-                    rhs=a_codes[:, c, HALF:N].bitcast(FP8X4),
-                    rhs_scale=a_scales[:, c, HALF:N],
-                    start=True,
-                    stop=True,
-                )
-
-        for i in range(UNITS):
-            leaky_relu(i)
-            if i == 1:
-                nc.vector.tensor_copy(out=c_32[:], in_=c_bf[:])
+        for i in range(A_UNITS):
             activation_unit(i)
+            if i == FIRST_W - 1:
+                nc.vector.tensor_copy(out=c_32[:], in_=c_bf[:])
             if i >= A_LAG:
-                quantise(i - A_LAG, a_grp[i - A_LAG], a_codes, a_scales)
-                if i - A_LAG >= UNITS - PASSES:
-                    warm_up(i - A_LAG - (UNITS - PASSES))
+                quantise_activation()
+            if i >= FIRST_W:
+                k = count["w_next"]
+                regroup_weighted(k, scale_rows(k))
+                multiply_if_ready()
+                count["step"] += 1
 
-        late = list(range(UNITS - A_LAG, UNITS))
-        for i in range(UNITS):
-            weighted = weighted_unit(i)
-            if late:
-                k = late.pop(0)
-                quantise(k, a_grp[k], a_codes, a_scales)
-                if k < UNITS - 1:
-                    warm_up(k - (UNITS - PASSES))
-            w_grp[i] = work.tile([P, BLK, PACK], BF16, name="w_grp", align_bytes=64)
-            regroup(i in WR_ON_VECTOR, w_grp[i], weighted[:])
-            if i >= W_LAG:
-                multiply(i - W_LAG, i)
+        while count["w_next"] < W_UNITS:
+            k = count["w_next"]
+            weighted = scale_rows(k)
+            if count["a_done"] < A_UNITS:
+                quantise_activation()
+            regroup_weighted(k, weighted)
+            multiply_if_ready()
             done = 0
-            while waiting and waiting[0][0] <= i - OUT_DELAY and done < OUT_PER_STEP:
+            while waiting and waiting[0][0] <= count["step"] - OUT_DELAY and done < OUT_PER_STEP:
                 finish(*waiting.pop(0)[1:])
                 done += 1
-        for i in range(UNITS - W_LAG, UNITS):
-            multiply(i, UNITS)
+            count["step"] += 1
+        while count["w_done"] < W_UNITS:
+            multiply(count["w_done"])
         while waiting:
             finish(*waiting.pop(0)[1:])

@@ -45,8 +45,9 @@ def tile_mnelayer_pb_kernel(tc, potential, contribution, out):
 
         c_bf = keep.tile([P, ROWS], BF16, name="c_bf")
         c_32 = keep.tile([P, ROWS], F32, name="c_32")
-        p_in = [keep.tile([P, PACK, N], BF16, name="p_in%d" % c) for c in range(PASSES)]
-        leaky = [keep.tile([P, PACK, N], F32, name="leaky%d" % c) for c in range(PASSES)]
+        p_first = [keep.tile([P, PACK, BLK], BF16, name="p_first%d" % q) for q in range(N // BLK)]
+        p_in = [keep.tile([P, PACK, N], BF16, name="p_in%d" % c) for c in range(1, PASSES)]
+        leaky = [keep.tile([P, PACK, HALF], F32, name="leaky%d" % i) for i in range(A_UNITS)]
         a_codes = keep.tile([P, PASSES, N], U32, name="a_codes", align_bytes=64)
         a_scales = keep.tile([P, PASSES, N], U8, name="a_scales", align_bytes=64)
         w_codes = keep.tile([P, PASSES, N], U32, name="w_codes", align_bytes=64)
@@ -57,16 +58,12 @@ def tile_mnelayer_pb_kernel(tc, potential, contribution, out):
             in_=contribution.rearrange("(c p j) -> p c j", c=PASSES, p=P),
         )
         for q in range(N // BLK):
-            cols = slice(BLK * q, BLK * (q + 1))
-            nc.sync.dma_start(out=p_in[0][:, :, cols], in_=pot[0][:, :, cols])
+            nc.sync.dma_start(out=p_first[q][:], in_=pot[0][:, :, BLK * q : BLK * (q + 1)])
         for c in range(1, PASSES):
-            nc.sync.dma_start(out=p_in[c][:], in_=pot[c])
+            nc.sync.dma_start(out=p_in[c - 1][:], in_=pot[c])
 
-        def leaky_relu(c, cols):
-            nc.vector.scalar_tensor_tensor(
-                out=leaky[c][:, :, cols], in0=p_in[c][:, :, cols], scalar=SLOPE, in1=p_in[c][:, :, cols],
-                op0=ALU.mult, op1=ALU.max,
-            )
+        def leaky_relu(dst, src):
+            nc.vector.scalar_tensor_tensor(out=dst, in0=src, scalar=SLOPE, in1=src, op0=ALU.mult, op1=ALU.max)
 
         def regroup(on_vector, dst, src):
             o = dst[:].rearrange("p (g i) j -> p g j i", i=4)
@@ -93,11 +90,11 @@ def tile_mnelayer_pb_kernel(tc, potential, contribution, out):
             c, h = divmod(i, 2)
             if c == 0:
                 for q in range(2):
-                    leaky_relu(c, slice(HALF * h + BLK * q, HALF * h + BLK * (q + 1)))
+                    leaky_relu(leaky[i][:, :, BLK * q : BLK * (q + 1)], p_first[2 * h + q][:])
             else:
-                leaky_relu(c, slice(HALF * h, HALF * (h + 1)))
+                leaky_relu(leaky[i][:], p_in[c - 1][:, :, HALF * h : HALF * (h + 1)])
             a_grp[i] = wide.tile([P, HALF, PACK], BF16, name="a_grp", align_bytes=64)
-            regroup(False, a_grp[i], leaky[c][:, :, HALF * h : HALF * (h + 1)])
+            regroup(False, a_grp[i], leaky[i][:])
 
         def quantise_activation():
             i = count["a_done"]
@@ -111,7 +108,7 @@ def tile_mnelayer_pb_kernel(tc, potential, contribution, out):
             for j in range(PACK):
                 r = PACK * c + j
                 nc.vector.tensor_scalar(
-                    out=weighted[:, j, :], in0=leaky[c][:, j, BLK * u : BLK * (u + 1)],
+                    out=weighted[:, j, :], in0=leaky[2 * c + u // 2][:, j, BLK * (u % 2) : BLK * (u % 2 + 1)],
                     scalar1=c_32[:, r : r + 1], scalar2=None, op0=ALU.mult,
                 )
             return weighted

@@ -26,8 +26,8 @@ FLOPS = 2 * B * N * N
 A_LAG = 2
 W_LAG = 2
 FIRST_W = 4
-WR_ON_VECTOR = (3, 7, 11)
-OUT_ON_VECTOR = ((0, 3), (1, 3), (2, 3), (3, 1), (3, 3))
+WR_ON_VECTOR = (2, 5, 7, 10, 13, 15)
+OUT_ON_VECTOR = ((3, 1), (3, 3))
 OUT_DELAY = 2
 OUT_PER_STEP = 2
 
@@ -40,6 +40,7 @@ def tile_mnelayer_pb_kernel(tc, potential, contribution, out):
         keep = ctx.enter_context(tc.tile_pool(name="keep", bufs=1))
         wide = ctx.enter_context(tc.tile_pool(name="wide", bufs=4))
         work = ctx.enter_context(tc.tile_pool(name="work", bufs=6))
+        outp = ctx.enter_context(tc.tile_pool(name="outp", bufs=16))
         psum = ctx.enter_context(tc.psum_pool(name="psum", bufs=8))
         ctx.enter_context(tc.manual_schedule())
 
@@ -104,6 +105,8 @@ def tile_mnelayer_pb_kernel(tc, potential, contribution, out):
 
         def scale_rows(k):
             u, c = divmod(k, PASSES)
+            if k in WR_ON_VECTOR:
+                return None
             weighted = work.tile([P, PACK, BLK], BF16, name="weighted")
             for j in range(PACK):
                 r = PACK * c + j
@@ -115,7 +118,16 @@ def tile_mnelayer_pb_kernel(tc, potential, contribution, out):
 
         def regroup_weighted(k, weighted):
             w_grp[k] = work.tile([P, BLK, PACK], BF16, name="w_grp", align_bytes=64)
-            regroup(k in WR_ON_VECTOR, w_grp[k], weighted[:])
+            if k in WR_ON_VECTOR:
+                u, c = divmod(k, PASSES)
+                nc.vector.tensor_tensor(
+                    out=w_grp[k][:].rearrange("p (g i) j -> p g j i", i=4),
+                    in0=leaky[2 * c + u // 2][:, :, BLK * (u % 2) : BLK * (u % 2 + 1)].rearrange("p j (g i) -> p g j i", i=4),
+                    in1=c_32[:, PACK * c : PACK * (c + 1)].unsqueeze(1).unsqueeze(3).to_broadcast([P, BLK // 4, PACK, 4]),
+                    op=ALU.mult,
+                )
+            else:
+                regroup(False, w_grp[k], weighted[:])
             count["w_next"] = k + 1
 
         def multiply(k):
@@ -146,7 +158,7 @@ def tile_mnelayer_pb_kernel(tc, potential, contribution, out):
                 multiply(k)
 
         def finish(u, m, h):
-            res = work.tile([P, HALF], F32, name="res")
+            res = outp.tile([P, HALF], F32, name="res")
             if (u, 2 * m + h) in OUT_ON_VECTOR:
                 nc.vector.tensor_scalar(out=res[:], in0=acc[(u, m, h)][:], scalar1=1.0 / B, scalar2=None, op0=ALU.mult)
             else:

@@ -19,15 +19,17 @@ ROWS = PASSES * PACK
 BLK = 256
 HALF = 512
 A_UNITS = PASSES * (N // HALF)
-W_UNITS = (N // BLK) * PASSES
+W_BLOCKS = ((0, 256), (256, 256), (512, 256), (768, 128), (896, 128))
+UNITS = tuple((col0, width, c) for col0, width in W_BLOCKS for c in range(PASSES))
+W_UNITS = len(UNITS)
 SLOPE = 0.01
 FLOPS = 2 * B * N * N
 
 A_LAG = 2
 W_LAG = 2
 FIRST_W = 4
-WR_ON_VECTOR = (2, 5, 7, 10, 13, 15)
-OUT_ON_VECTOR = ((3, 1), (3, 3))
+WR_ON_VECTOR = (5, 7, 10, 13, 14, 15, 17, 18, 19)
+OUT_ON_VECTOR = ((7, 1),)
 OUT_DELAY = 2
 OUT_PER_STEP = 2
 
@@ -104,26 +106,26 @@ def tile_mnelayer_pb_kernel(tc, potential, contribution, out):
             count["a_done"] = i + 1
 
         def scale_rows(k):
-            u, c = divmod(k, PASSES)
+            col0, width, c = UNITS[k]
             if k in WR_ON_VECTOR:
                 return None
-            weighted = work.tile([P, PACK, BLK], BF16, name="weighted")
+            weighted = work.tile([P, PACK, width], BF16, name="weighted")
             for j in range(PACK):
                 r = PACK * c + j
                 nc.vector.tensor_scalar(
-                    out=weighted[:, j, :], in0=leaky[2 * c + u // 2][:, j, BLK * (u % 2) : BLK * (u % 2 + 1)],
+                    out=weighted[:, j, :], in0=leaky[2 * c + col0 // HALF][:, j, col0 % HALF : col0 % HALF + width],
                     scalar1=c_32[:, r : r + 1], scalar2=None, op0=ALU.mult,
                 )
             return weighted
 
         def regroup_weighted(k, weighted):
-            w_grp[k] = work.tile([P, BLK, PACK], BF16, name="w_grp", align_bytes=64)
+            col0, width, c = UNITS[k]
+            w_grp[k] = work.tile([P, width, PACK], BF16, name="w_grp", align_bytes=64)
             if k in WR_ON_VECTOR:
-                u, c = divmod(k, PASSES)
                 nc.vector.tensor_tensor(
                     out=w_grp[k][:].rearrange("p (g i) j -> p g j i", i=4),
-                    in0=leaky[2 * c + u // 2][:, :, BLK * (u % 2) : BLK * (u % 2 + 1)].rearrange("p j (g i) -> p g j i", i=4),
-                    in1=c_32[:, PACK * c : PACK * (c + 1)].unsqueeze(1).unsqueeze(3).to_broadcast([P, BLK // 4, PACK, 4]),
+                    in0=leaky[2 * c + col0 // HALF][:, :, col0 % HALF : col0 % HALF + width].rearrange("p j (g i) -> p g j i", i=4),
+                    in1=c_32[:, PACK * c : PACK * (c + 1)].unsqueeze(1).unsqueeze(3).to_broadcast([P, width // 4, PACK, 4]),
                     op=ALU.mult,
                 )
             else:
@@ -131,16 +133,16 @@ def tile_mnelayer_pb_kernel(tc, potential, contribution, out):
             count["w_next"] = k + 1
 
         def multiply(k):
-            u, c = divmod(k, PASSES)
-            quantise(w_grp[k], w_codes, w_scales, c, slice(BLK * u, BLK * (u + 1)))
-            for m in range(2):
+            col0, width, c = UNITS[k]
+            quantise(w_grp[k], w_codes, w_scales, c, slice(col0, col0 + width))
+            for m in range(col0 // P, (col0 + width) // P):
                 for h in range(2):
                     if c == 0:
-                        acc[(u, m, h)] = psum.tile([P, HALF], F32, name="acc")
-                    lcols = slice(BLK * u + P * m, BLK * u + P * (m + 1))
+                        acc[(m, h)] = psum.tile([P, HALF], F32, name="acc")
+                    lcols = slice(P * m, P * (m + 1))
                     rcols = slice(HALF * h, HALF * (h + 1))
                     nc.tensor.matmul_mx(
-                        out=acc[(u, m, h)][:],
+                        out=acc[(m, h)][:],
                         lhsT=w_codes[:, c, lcols].bitcast(FP8X4),
                         lhsT_scale=w_scales[:, c, lcols],
                         rhs=a_codes[:, c, rcols].bitcast(FP8X4),
@@ -149,33 +151,32 @@ def tile_mnelayer_pb_kernel(tc, potential, contribution, out):
                         stop=(c == PASSES - 1),
                     )
                     if c == PASSES - 1:
-                        waiting.append((count["step"], u, m, h))
+                        waiting.append((count["step"], m, h))
             count["w_done"] = k + 1
 
-        def multiply_if_ready():
+        def multiply_if_ready(lag=W_LAG):
             k = count["w_done"]
-            if count["w_next"] - k > W_LAG and count["a_done"] >= 2 * (k % PASSES) + 2:
+            if count["w_next"] - k > lag and count["a_done"] >= 2 * UNITS[k][2] + 2:
                 multiply(k)
 
-        def finish(u, m, h):
+        def finish(m, h):
             res = outp.tile([P, HALF], F32, name="res")
-            if (u, 2 * m + h) in OUT_ON_VECTOR:
-                nc.vector.tensor_scalar(out=res[:], in0=acc[(u, m, h)][:], scalar1=1.0 / B, scalar2=None, op0=ALU.mult)
+            if (m, h) in OUT_ON_VECTOR:
+                nc.vector.tensor_scalar(out=res[:], in0=acc[(m, h)][:], scalar1=1.0 / B, scalar2=None, op0=ALU.mult)
             else:
-                nc.scalar.activation(out=res[:], in_=acc[(u, m, h)][:], func=ACT.Copy, scale=1.0 / B)
-            row0 = BLK * u + P * m
-            nc.sync.dma_start(out=out[row0 : row0 + P, HALF * h : HALF * (h + 1)], in_=res[:])
+                nc.scalar.activation(out=res[:], in_=acc[(m, h)][:], func=ACT.Copy, scale=1.0 / B)
+            nc.sync.dma_start(out=out[P * m : P * (m + 1), HALF * h : HALF * (h + 1)], in_=res[:])
 
         for i in range(A_UNITS):
             activation_unit(i)
-            if i == FIRST_W - 1:
+            if i == 1:
                 nc.vector.tensor_copy(out=c_32[:], in_=c_bf[:])
             if i >= A_LAG:
                 quantise_activation()
-            if i >= FIRST_W:
+            if i % 2 == 1:
                 k = count["w_next"]
                 regroup_weighted(k, scale_rows(k))
-                multiply_if_ready()
+                multiply_if_ready(1)
                 count["step"] += 1
 
         while count["w_next"] < W_UNITS:

@@ -28,7 +28,7 @@ FLOPS = 2 * B * N * N
 A_LAG = 2
 W_LAG = 2
 FIRST_W = 4
-WR_ON_VECTOR = (5, 7, 10, 13, 14, 15, 17, 18, 19)
+WR_ON_VECTOR = (5, 7, 9, 11, 12, 13, 14, 15, 16, 17, 18, 19)
 OUT_ON_VECTOR = ((7, 1),)
 OUT_DELAY = 2
 OUT_PER_STEP = 2

@@ -1,6 +1,7 @@
 from contextlib import ExitStack
 
 import concourse.mybir as mybir
+from concourse.masks import make_identity
 
 F32 = mybir.dt.float32
 BF16 = mybir.dt.bfloat16
@@ -16,22 +17,18 @@ N = 1024
 PACK = 4
 PASSES = B // (P * PACK)
 ROWS = PASSES * PACK
-BLK = 256
 HALF = 512
-A_UNITS = PASSES * (N // HALF)
-W_BLOCKS = ((0, 256), (256, 256), (512, 256), (768, 128), (896, 128))
-UNITS = tuple((col0, width, c) for col0, width in W_BLOCKS for c in range(PASSES))
-W_UNITS = len(UNITS)
+QUART = 256
 SLOPE = 0.01
 FLOPS = 2 * B * N * N
 
-A_LAG = 2
-W_LAG = 2
-FIRST_W = 4
-WR_ON_VECTOR = (5, 7, 9, 11, 12, 13, 14, 15, 16, 17, 18, 19)
-OUT_ON_VECTOR = ((7, 1),)
-OUT_DELAY = 2
-OUT_PER_STEP = 2
+LAST = PASSES - 1
+LEFT, RIGHT = 0, 1
+LEFT_TILES = (0, 1, 2, 3)
+RIGHT_TILES = (4, 5, 6, 7)
+LATE_TILES = (6, 7)
+EARLY_TILES = (0, 1, 2, 3, 4, 5)
+TILES = LEFT_TILES + RIGHT_TILES
 
 
 def tile_mnelayer_pb_kernel(tc, potential, contribution, out):
@@ -40,17 +37,23 @@ def tile_mnelayer_pb_kernel(tc, potential, contribution, out):
 
     with ExitStack() as ctx:
         keep = ctx.enter_context(tc.tile_pool(name="keep", bufs=1))
-        wide = ctx.enter_context(tc.tile_pool(name="wide", bufs=4))
-        work = ctx.enter_context(tc.tile_pool(name="work", bufs=6))
-        outp = ctx.enter_context(tc.tile_pool(name="outp", bufs=16))
-        psum = ctx.enter_context(tc.psum_pool(name="psum", bufs=8))
+        work = ctx.enter_context(tc.tile_pool(name="work", bufs=3))
+        groups = ctx.enter_context(tc.tile_pool(name="groups", bufs=5))
+        outp = ctx.enter_context(tc.tile_pool(name="outp", bufs=8))
+        psum = ctx.enter_context(tc.psum_pool(name="psum", bufs=6))
+        late = ctx.enter_context(tc.psum_pool(name="late", bufs=2))
         ctx.enter_context(tc.manual_schedule())
 
         c_bf = keep.tile([P, ROWS], BF16, name="c_bf")
         c_32 = keep.tile([P, ROWS], F32, name="c_32")
-        p_first = [keep.tile([P, PACK, BLK], BF16, name="p_first%d" % q) for q in range(N // BLK)]
+        c_neg = keep.tile([P, ROWS], F32, name="c_neg")
+        ident = keep.tile([P, P], BF16, name="ident")
+        first = [keep.tile([P, PACK, QUART], BF16, name="first%d" % q) for q in range(2)]
+        right0 = keep.tile([P, PACK, HALF], BF16, name="right0")
         p_in = [keep.tile([P, PACK, N], BF16, name="p_in%d" % c) for c in range(1, PASSES)]
-        leaky = [keep.tile([P, PACK, HALF], F32, name="leaky%d" % i) for i in range(A_UNITS)]
+        leaky = {}
+        for c, h in ((0, LEFT), (1, LEFT), (2, LEFT), (3, LEFT), (LAST, RIGHT)):
+            leaky[(c, h)] = keep.tile([P, PACK, HALF], F32, name="leaky%d%d" % (c, h))
         a_codes = keep.tile([P, PASSES, N], U32, name="a_codes", align_bytes=64)
         a_scales = keep.tile([P, PASSES, N], U8, name="a_scales", align_bytes=64)
         w_codes = keep.tile([P, PASSES, N], U32, name="w_codes", align_bytes=64)
@@ -60,23 +63,27 @@ def tile_mnelayer_pb_kernel(tc, potential, contribution, out):
             out=c_bf[:].rearrange("p (c j) -> p c j", j=PACK),
             in_=contribution.rearrange("(c p j) -> p c j", c=PASSES, p=P),
         )
-        for q in range(N // BLK):
-            nc.sync.dma_start(out=p_first[q][:], in_=pot[0][:, :, BLK * q : BLK * (q + 1)])
+        for q in range(2):
+            nc.sync.dma_start(out=first[q][:], in_=pot[0][:, :, QUART * q : QUART * (q + 1)])
+        nc.sync.dma_start(out=right0[:], in_=pot[0][:, :, HALF:N])
         for c in range(1, PASSES):
             nc.sync.dma_start(out=p_in[c - 1][:], in_=pot[c])
+        make_identity(nc, ident[:])
+
+        def right_half(c):
+            return right0[:] if c == 0 else p_in[c - 1][:, :, HALF:N]
+
+        def grouped(dst):
+            return dst.rearrange("p (g i) j -> p g j i", i=4)
+
+        def rows_of(src):
+            return src.rearrange("p j (g i) -> p g j i", i=4)
 
         def leaky_relu(dst, src):
             nc.vector.scalar_tensor_tensor(out=dst, in0=src, scalar=SLOPE, in1=src, op0=ALU.mult, op1=ALU.max)
 
-        def regroup(on_vector, dst, src):
-            o = dst[:].rearrange("p (g i) j -> p g j i", i=4)
-            s = src.rearrange("p j (g i) -> p g j i", i=4)
-            if on_vector:
-                nc.vector.tensor_copy(out=o, in_=s)
-            else:
-                nc.scalar.copy(out=o, in_=s)
-
-        def quantise(grp, codes, scales, c, cols):
+        def quantise(grp, codes, scales, c, col0, width):
+            cols = slice(col0, col0 + width)
             nc.vector.quantize_mx(
                 out=codes[:, c, cols].bitcast(FP8X4),
                 scales=scales[:, c, cols],
@@ -86,112 +93,170 @@ def tile_mnelayer_pb_kernel(tc, potential, contribution, out):
         a_grp = {}
         w_grp = {}
         acc = {}
-        waiting = []
-        count = {"a_done": 0, "w_next": 0, "w_done": 0, "step": 0}
+        done = {}
 
-        def activation_unit(i):
-            c, h = divmod(i, 2)
-            if c == 0:
+        def leak(c, h):
+            if (c, h) == (0, LEFT):
                 for q in range(2):
-                    leaky_relu(leaky[i][:, :, BLK * q : BLK * (q + 1)], p_first[2 * h + q][:])
+                    leaky_relu(leaky[(0, LEFT)][:, :, QUART * q : QUART * (q + 1)], first[q][:])
+            elif h == LEFT:
+                leaky_relu(leaky[(c, h)][:], p_in[c - 1][:, :, 0:HALF])
             else:
-                leaky_relu(leaky[i][:], p_in[c - 1][:, :, HALF * h : HALF * (h + 1)])
-            a_grp[i] = wide.tile([P, HALF, PACK], BF16, name="a_grp", align_bytes=64)
-            regroup(False, a_grp[i], leaky[i][:])
+                leaky_relu(leaky[(c, h)][:], right_half(c))
 
-        def quantise_activation():
-            i = count["a_done"]
-            c, h = divmod(i, 2)
-            quantise(a_grp[i], a_codes, a_scales, c, slice(HALF * h, HALF * (h + 1)))
-            count["a_done"] = i + 1
+        def regroup_a(c, h):
+            a_grp[(c, h)] = groups.tile([P, HALF, PACK], BF16, name="a_grp", align_bytes=64)
+            pieces = 2 if (c, h) == (0, LEFT) else 1
+            width = HALF // pieces
+            for q in range(pieces):
+                cols = slice(width * q, width * (q + 1))
+                nc.scalar.copy(out=grouped(a_grp[(c, h)][:, cols, :]), in_=rows_of(leaky[(c, h)][:, :, cols]))
 
-        def scale_rows(k):
-            col0, width, c = UNITS[k]
-            if k in WR_ON_VECTOR:
-                return None
-            weighted = work.tile([P, PACK, width], BF16, name="weighted")
+        def quantise_a(c, h):
+            quantise(a_grp[(c, h)], a_codes, a_scales, c, HALF * h, HALF)
+
+        def direct_a(c, q):
+            a_grp[(c, "q", q)] = groups.tile([P, QUART, PACK], BF16, name="d_grp", align_bytes=64)
+            x = right_half(c)[:, :, QUART * q : QUART * (q + 1)]
+            leaky_relu(a_grp[(c, "q", q)][:], x.rearrange("p j w -> p w j"))
+
+        def quantise_direct(c, q):
+            quantise(a_grp[(c, "q", q)], a_codes, a_scales, c, HALF + QUART * q, QUART)
+
+        def scale(c, h):
+            weighted = work.tile([P, PACK, HALF], BF16, name="weighted")
             for j in range(PACK):
                 r = PACK * c + j
                 nc.vector.tensor_scalar(
-                    out=weighted[:, j, :], in0=leaky[2 * c + col0 // HALF][:, j, col0 % HALF : col0 % HALF + width],
+                    out=weighted[:, j, :], in0=leaky[(c, h)][:, j, :],
                     scalar1=c_32[:, r : r + 1], scalar2=None, op0=ALU.mult,
                 )
-            return weighted
+            w_grp[(c, h)] = groups.tile([P, HALF, PACK], BF16, name="w_grp", align_bytes=64)
+            nc.scalar.copy(out=grouped(w_grp[(c, h)][:]), in_=rows_of(weighted[:]))
 
-        def regroup_weighted(k, weighted):
-            col0, width, c = UNITS[k]
-            w_grp[k] = work.tile([P, width, PACK], BF16, name="w_grp", align_bytes=64)
-            if k in WR_ON_VECTOR:
-                nc.vector.tensor_tensor(
-                    out=w_grp[k][:].rearrange("p (g i) j -> p g j i", i=4),
-                    in0=leaky[2 * c + col0 // HALF][:, :, col0 % HALF : col0 % HALF + width].rearrange("p j (g i) -> p g j i", i=4),
-                    in1=c_32[:, PACK * c : PACK * (c + 1)].unsqueeze(1).unsqueeze(3).to_broadcast([P, width // 4, PACK, 4]),
-                    op=ALU.mult,
+        def branches(c):
+            pos = work.tile([P, PACK, HALF], BF16, name="pos")
+            neg = work.tile([P, PACK, HALF], BF16, name="neg")
+            x = right_half(c)
+            for j in range(PACK):
+                r = PACK * c + j
+                nc.vector.tensor_scalar(
+                    out=pos[:, j, :], in0=x[:, j, :], scalar1=0.0, scalar2=c_32[:, r : r + 1], op0=ALU.max, op1=ALU.mult,
                 )
+                nc.vector.tensor_scalar(
+                    out=neg[:, j, :], in0=x[:, j, :], scalar1=0.0, scalar2=c_neg[:, r : r + 1], op0=ALU.min, op1=ALU.mult,
+                )
+            w_grp[(c, RIGHT)] = groups.tile([P, HALF, PACK], BF16, name="w_grp", align_bytes=64)
+            for q in range(2):
+                bank = late.tile([P, PACK * QUART], BF16, name="bank")
+                for s in range(2):
+                    cols = slice(QUART * q + P * s, QUART * q + P * (s + 1))
+                    half_bank = bank[:, HALF * s : HALF * (s + 1)]
+                    nc.tensor.matmul(out=half_bank, lhsT=ident[:], rhs=pos[:, :, cols].rearrange("p j w -> p w j"), start=True, stop=False)
+                    nc.tensor.matmul(out=half_bank, lhsT=ident[:], rhs=neg[:, :, cols].rearrange("p j w -> p w j"), start=False, stop=True)
+                nc.scalar.copy(
+                    out=w_grp[(c, RIGHT)][:, QUART * q : QUART * (q + 1), :].rearrange("p w j -> p (w j)"), in_=bank[:],
+                )
+
+        def quantise_w(c, h):
+            quantise(w_grp[(c, h)], w_codes, w_scales, c, HALF * h, HALF)
+
+        def multiply(m, c, col0, width):
+            if (m, col0) not in acc:
+                if m in LATE_TILES:
+                    acc[(m, col0)] = late.tile([P, HALF], F32, name="bank")
+                else:
+                    acc[(m, col0)] = psum.tile([P, HALF], F32, name="acc")
+            done[(m, col0)] = done.get((m, col0), 0) + 1
+            lcols = slice(P * m, P * (m + 1))
+            rcols = slice(col0, col0 + width)
+            nc.tensor.matmul_mx(
+                out=acc[(m, col0)][:, 0:width],
+                lhsT=w_codes[:, c, lcols].bitcast(FP8X4),
+                lhsT_scale=w_scales[:, c, lcols],
+                rhs=a_codes[:, c, rcols].bitcast(FP8X4),
+                rhs_scale=a_scales[:, c, rcols],
+                start=done[(m, col0)] == 1,
+                stop=done[(m, col0)] == PASSES,
+            )
+
+        def multiply_left(tiles, c):
+            for m in tiles:
+                multiply(m, c, 0, HALF)
+
+        def finish(m, col0, width, on_vector=False):
+            res = outp.tile([P, width], F32, name="res%d" % width)
+            src = acc[(m, col0)][:, 0:width]
+            if on_vector:
+                nc.vector.tensor_scalar(out=res[:], in0=src, scalar1=1.0 / B, scalar2=None, op0=ALU.mult)
             else:
-                regroup(False, w_grp[k], weighted[:])
-            count["w_next"] = k + 1
+                nc.scalar.activation(out=res[:], in_=src, func=ACT.Copy, scale=1.0 / B)
+            nc.sync.dma_start(out=out[P * m : P * (m + 1), col0 : col0 + width], in_=res[:])
 
-        def multiply(k):
-            col0, width, c = UNITS[k]
-            quantise(w_grp[k], w_codes, w_scales, c, slice(col0, col0 + width))
-            for m in range(col0 // P, (col0 + width) // P):
-                for h in range(2):
-                    if c == 0:
-                        acc[(m, h)] = psum.tile([P, HALF], F32, name="acc")
-                    lcols = slice(P * m, P * (m + 1))
-                    rcols = slice(HALF * h, HALF * (h + 1))
-                    nc.tensor.matmul_mx(
-                        out=acc[(m, h)][:],
-                        lhsT=w_codes[:, c, lcols].bitcast(FP8X4),
-                        lhsT_scale=w_scales[:, c, lcols],
-                        rhs=a_codes[:, c, rcols].bitcast(FP8X4),
-                        rhs_scale=a_scales[:, c, rcols],
-                        start=(c == 0),
-                        stop=(c == PASSES - 1),
-                    )
-                    if c == PASSES - 1:
-                        waiting.append((count["step"], m, h))
-            count["w_done"] = k + 1
+        leak(0, LEFT)
+        regroup_a(0, LEFT)
+        nc.vector.tensor_copy(out=c_32[:], in_=c_bf[:])
+        nc.vector.tensor_scalar(out=c_neg[:], in0=c_bf[:], scalar1=SLOPE, scalar2=None, op0=ALU.mult)
+        scale(0, LEFT)
+        branches(0)
+        leak(1, LEFT)
+        regroup_a(1, LEFT)
+        branches(1)
+        scale(1, LEFT)
+        leak(2, LEFT)
+        regroup_a(2, LEFT)
+        quantise_a(0, LEFT)
+        quantise_w(0, RIGHT)
+        quantise_w(0, LEFT)
+        multiply_left(EARLY_TILES, 0)
+        leak(3, LEFT)
+        regroup_a(3, LEFT)
+        branches(2)
+        scale(2, LEFT)
+        quantise_a(1, LEFT)
+        quantise_w(1, RIGHT)
+        quantise_w(1, LEFT)
+        multiply_left(EARLY_TILES, 1)
+        scale(3, LEFT)
+        multiply_left(LATE_TILES, 0)
+        multiply_left(LATE_TILES, 1)
+        leak(LAST, RIGHT)
+        quantise_a(2, LEFT)
+        quantise_w(2, RIGHT)
+        multiply_left(RIGHT_TILES, 2)
+        scale(LAST, RIGHT)
+        regroup_a(LAST, RIGHT)
+        quantise_w(2, LEFT)
+        multiply_left(LEFT_TILES, 2)
+        quantise_a(3, LEFT)
+        quantise_w(3, LEFT)
+        multiply_left(LEFT_TILES, 3)
+        direct_a(0, 0)
+        quantise_w(3, RIGHT)
+        multiply_left(RIGHT_TILES, 3)
+        for m in TILES:
+            finish(m, 0, HALF)
 
-        def multiply_if_ready(lag=W_LAG):
-            k = count["w_done"]
-            if count["w_next"] - k > lag and count["a_done"] >= 2 * UNITS[k][2] + 2:
-                multiply(k)
+        direct_a(1, 0)
+        quantise_direct(0, 0)
+        direct_a(2, 0)
+        quantise_direct(1, 0)
+        quantise_a(LAST, RIGHT)
+        quantise_direct(2, 0)
+        for m in TILES:
+            for c in range(PASSES):
+                multiply(m, c, HALF, QUART)
 
-        def finish(m, h):
-            res = outp.tile([P, HALF], F32, name="res")
-            if (m, h) in OUT_ON_VECTOR:
-                nc.vector.tensor_scalar(out=res[:], in0=acc[(m, h)][:], scalar1=1.0 / B, scalar2=None, op0=ALU.mult)
-            else:
-                nc.scalar.activation(out=res[:], in_=acc[(m, h)][:], func=ACT.Copy, scale=1.0 / B)
-            nc.sync.dma_start(out=out[P * m : P * (m + 1), HALF * h : HALF * (h + 1)], in_=res[:])
-
-        for i in range(A_UNITS):
-            activation_unit(i)
-            if i == 1:
-                nc.vector.tensor_copy(out=c_32[:], in_=c_bf[:])
-            if i >= A_LAG:
-                quantise_activation()
-            if i % 2 == 1:
-                k = count["w_next"]
-                regroup_weighted(k, scale_rows(k))
-                multiply_if_ready(1)
-                count["step"] += 1
-
-        while count["w_next"] < W_UNITS:
-            k = count["w_next"]
-            weighted = scale_rows(k)
-            if count["a_done"] < A_UNITS:
-                quantise_activation()
-            regroup_weighted(k, weighted)
-            multiply_if_ready()
-            done = 0
-            while waiting and waiting[0][0] <= count["step"] - OUT_DELAY and done < OUT_PER_STEP:
-                finish(*waiting.pop(0)[1:])
-                done += 1
-            count["step"] += 1
-        while count["w_done"] < W_UNITS:
-            multiply(count["w_done"])
-        while waiting:
-            finish(*waiting.pop(0)[1:])
+        direct_a(0, 1)
+        direct_a(1, 1)
+        quantise_direct(0, 1)
+        direct_a(2, 1)
+        quantise_direct(1, 1)
+        quantise_direct(2, 1)
+        for m in TILES:
+            finish(m, HALF, QUART)
+        for m in TILES:
+            for c in range(PASSES):
+                multiply(m, c, HALF + QUART, QUART)
+        for i, m in enumerate(TILES):
+            finish(m, HALF + QUART, QUART, i % 2 == 0)

@@ -92,6 +92,7 @@ def tile_mnelayer_pb_kernel(tc, potential, contribution, out):
 
         a_grp = {}
         w_grp = {}
+        banks = {}
         acc = {}
         done = {}
 
@@ -151,11 +152,15 @@ def tile_mnelayer_pb_kernel(tc, potential, contribution, out):
                 bank = late.tile([P, PACK * QUART], BF16, name="bank")
                 for s in range(2):
                     cols = slice(QUART * q + P * s, QUART * q + P * (s + 1))
-                    half_bank = bank[:, HALF * s : HALF * (s + 1)]
-                    nc.tensor.matmul(out=half_bank, lhsT=ident[:], rhs=pos[:, :, cols].rearrange("p j w -> p w j"), start=True, stop=False)
-                    nc.tensor.matmul(out=half_bank, lhsT=ident[:], rhs=neg[:, :, cols].rearrange("p j w -> p w j"), start=False, stop=True)
+                    half_bank = grouped(bank[:, HALF * s : HALF * (s + 1)].rearrange("p (w j) -> p w j", j=PACK))
+                    nc.tensor.matmul(out=half_bank, lhsT=ident[:], rhs=rows_of(pos[:, :, cols]), start=True, stop=False)
+                    nc.tensor.matmul(out=half_bank, lhsT=ident[:], rhs=rows_of(neg[:, :, cols]), start=False, stop=True)
+                banks[(c, q)] = bank
+
+        def collect(c):
+            for q in range(2):
                 nc.scalar.copy(
-                    out=w_grp[(c, RIGHT)][:, QUART * q : QUART * (q + 1), :].rearrange("p w j -> p (w j)"), in_=bank[:],
+                    out=w_grp[(c, RIGHT)][:, QUART * q : QUART * (q + 1), :].rearrange("p w j -> p (w j)"), in_=banks[(c, q)][:],
                 )
 
         def quantise_w(c, h):
@@ -201,8 +206,10 @@ def tile_mnelayer_pb_kernel(tc, potential, contribution, out):
         branches(0)
         leak(1, LEFT)
         regroup_a(1, LEFT)
+        collect(0)
         branches(1)
         scale(1, LEFT)
+        collect(1)
         leak(2, LEFT)
         regroup_a(2, LEFT)
         quantise_a(0, LEFT)
@@ -213,6 +220,7 @@ def tile_mnelayer_pb_kernel(tc, potential, contribution, out):
         regroup_a(3, LEFT)
         branches(2)
         scale(2, LEFT)
+        collect(2)
         quantise_a(1, LEFT)
         quantise_w(1, RIGHT)
         quantise_w(1, LEFT)

@@ -73,11 +73,11 @@ def tile_mnelayer_pb_kernel(tc, potential, contribution, out):
         def right_half(c):
             return right0[:] if c == 0 else p_in[c - 1][:, :, HALF:N]
 
-        def grouped(dst):
-            return dst.rearrange("p (g i) j -> p g j i", i=4)
+        def grouped(dst, run=4):
+            return dst.rearrange("p (g i) j -> p g j i", i=run)
 
-        def rows_of(src):
-            return src.rearrange("p j (g i) -> p g j i", i=4)
+        def rows_of(src, run=4):
+            return src.rearrange("p j (g i) -> p g j i", i=run)
 
         def leaky_relu(dst, src):
             nc.vector.scalar_tensor_tensor(out=dst, in0=src, scalar=SLOPE, in1=src, op0=ALU.mult, op1=ALU.max)
@@ -133,7 +133,7 @@ def tile_mnelayer_pb_kernel(tc, potential, contribution, out):
                     scalar1=c_32[:, r : r + 1], scalar2=None, op0=ALU.mult,
                 )
             w_grp[(c, h)] = groups.tile([P, HALF, PACK], BF16, name="w_grp", align_bytes=64)
-            nc.scalar.copy(out=grouped(w_grp[(c, h)][:]), in_=rows_of(weighted[:]))
+            nc.scalar.copy(out=grouped(w_grp[(c, h)][:], 8), in_=rows_of(weighted[:], 8))
 
         def branches(c):
             pos = work.tile([P, PACK, HALF], BF16, name="pos")
@@ -152,9 +152,9 @@ def tile_mnelayer_pb_kernel(tc, potential, contribution, out):
                 bank = late.tile([P, PACK * QUART], BF16, name="bank")
                 for s in range(2):
                     cols = slice(QUART * q + P * s, QUART * q + P * (s + 1))
-                    half_bank = grouped(bank[:, HALF * s : HALF * (s + 1)].rearrange("p (w j) -> p w j", j=PACK))
-                    nc.tensor.matmul(out=half_bank, lhsT=ident[:], rhs=rows_of(pos[:, :, cols]), start=True, stop=False)
-                    nc.tensor.matmul(out=half_bank, lhsT=ident[:], rhs=rows_of(neg[:, :, cols]), start=False, stop=True)
+                    half_bank = grouped(bank[:, HALF * s : HALF * (s + 1)].rearrange("p (w j) -> p w j", j=PACK), 8)
+                    nc.tensor.matmul(out=half_bank, lhsT=ident[:], rhs=rows_of(pos[:, :, cols], 8), start=True, stop=False)
+                    nc.tensor.matmul(out=half_bank, lhsT=ident[:], rhs=rows_of(neg[:, :, cols], 8), start=False, stop=True)
                 banks[(c, q)] = bank
 
         def collect(c):

@@ -26,8 +26,7 @@ LAST = PASSES - 1
 LEFT, RIGHT = 0, 1
 LEFT_TILES = (0, 1, 2, 3)
 RIGHT_TILES = (4, 5, 6, 7)
-LATE_TILES = (6, 7)
-EARLY_TILES = (0, 1, 2, 3, 4, 5)
+HEAD_PIECES = ((0, 128), (128, 128), (256, 256))
 TILES = LEFT_TILES + RIGHT_TILES
 
 
@@ -40,15 +39,14 @@ def tile_mnelayer_pb_kernel(tc, potential, contribution, out):
         work = ctx.enter_context(tc.tile_pool(name="work", bufs=3))
         groups = ctx.enter_context(tc.tile_pool(name="groups", bufs=5))
         outp = ctx.enter_context(tc.tile_pool(name="outp", bufs=8))
-        psum = ctx.enter_context(tc.psum_pool(name="psum", bufs=6))
-        late = ctx.enter_context(tc.psum_pool(name="late", bufs=2))
+        psum = ctx.enter_context(tc.psum_pool(name="psum", bufs=8))
         ctx.enter_context(tc.manual_schedule())
 
         c_bf = keep.tile([P, ROWS], BF16, name="c_bf")
         c_32 = keep.tile([P, ROWS], F32, name="c_32")
         c_neg = keep.tile([P, ROWS], F32, name="c_neg")
         ident = keep.tile([P, P], BF16, name="ident")
-        first = [keep.tile([P, PACK, QUART], BF16, name="first%d" % q) for q in range(2)]
+        first = [keep.tile([P, PACK, width], BF16, name="first%d" % col0) for col0, width in HEAD_PIECES]
         right0 = keep.tile([P, PACK, HALF], BF16, name="right0")
         p_in = [keep.tile([P, PACK, N], BF16, name="p_in%d" % c) for c in range(1, PASSES)]
         leaky = {}
@@ -63,8 +61,8 @@ def tile_mnelayer_pb_kernel(tc, potential, contribution, out):
             out=c_bf[:].rearrange("p (c j) -> p c j", j=PACK),
             in_=contribution.rearrange("(c p j) -> p c j", c=PASSES, p=P),
         )
-        for q in range(2):
-            nc.sync.dma_start(out=first[q][:], in_=pot[0][:, :, QUART * q : QUART * (q + 1)])
+        for (col0, width), piece in zip(HEAD_PIECES, first):
+            nc.sync.dma_start(out=piece[:], in_=pot[0][:, :, col0 : col0 + width])
         nc.sync.dma_start(out=right0[:], in_=pot[0][:, :, HALF:N])
         for c in range(1, PASSES):
             nc.sync.dma_start(out=p_in[c - 1][:], in_=pot[c])
@@ -98,8 +96,8 @@ def tile_mnelayer_pb_kernel(tc, potential, contribution, out):
 
         def leak(c, h):
             if (c, h) == (0, LEFT):
-                for q in range(2):
-                    leaky_relu(leaky[(0, LEFT)][:, :, QUART * q : QUART * (q + 1)], first[q][:])
+                for (col0, width), piece in zip(HEAD_PIECES, first):
+                    leaky_relu(leaky[(0, LEFT)][:, :, col0 : col0 + width], piece[:])
             elif h == LEFT:
                 leaky_relu(leaky[(c, h)][:], p_in[c - 1][:, :, 0:HALF])
             else:
@@ -107,10 +105,8 @@ def tile_mnelayer_pb_kernel(tc, potential, contribution, out):
 
         def regroup_a(c, h):
             a_grp[(c, h)] = groups.tile([P, HALF, PACK], BF16, name="a_grp", align_bytes=64)
-            pieces = 2 if (c, h) == (0, LEFT) else 1
-            width = HALF // pieces
-            for q in range(pieces):
-                cols = slice(width * q, width * (q + 1))
+            for col0, width in HEAD_PIECES if (c, h) == (0, LEFT) else ((0, HALF),):
+                cols = slice(col0, col0 + width)
                 nc.scalar.copy(out=grouped(a_grp[(c, h)][:, cols, :]), in_=rows_of(leaky[(c, h)][:, :, cols]))
 
         def quantise_a(c, h):
@@ -149,7 +145,7 @@ def tile_mnelayer_pb_kernel(tc, potential, contribution, out):
                 )
             w_grp[(c, RIGHT)] = groups.tile([P, HALF, PACK], BF16, name="w_grp", align_bytes=64)
             for q in range(2):
-                bank = late.tile([P, PACK * QUART], BF16, name="bank")
+                bank = psum.tile([P, PACK * QUART], BF16, name="bank")
                 for s in range(2):
                     cols = slice(QUART * q + P * s, QUART * q + P * (s + 1))
                     half_bank = grouped(bank[:, HALF * s : HALF * (s + 1)].rearrange("p (w j) -> p w j", j=PACK), 8)
@@ -168,10 +164,7 @@ def tile_mnelayer_pb_kernel(tc, potential, contribution, out):
 
         def multiply(m, c, col0, width):
             if (m, col0) not in acc:
-                if m in LATE_TILES:
-                    acc[(m, col0)] = late.tile([P, HALF], F32, name="bank")
-                else:
-                    acc[(m, col0)] = psum.tile([P, HALF], F32, name="acc")
+                acc[(m, col0)] = psum.tile([P, HALF], F32, name="bank")
             done[(m, col0)] = done.get((m, col0), 0) + 1
             lcols = slice(P * m, P * (m + 1))
             rcols = slice(col0, col0 + width)
@@ -185,9 +178,14 @@ def tile_mnelayer_pb_kernel(tc, potential, contribution, out):
                 stop=done[(m, col0)] == PASSES,
             )
 
-        def multiply_left(tiles, c):
+        def multiply_tiles(tiles, passes, col0, width):
+            for c in passes:
+                for m in tiles:
+                    multiply(m, c, col0, width)
+
+        def multiply_by_tile(tiles, passes, col0, width):
             for m in tiles:
-                multiply(m, c, 0, HALF)
+                multiply_tiles((m,), passes, col0, width)
 
         def finish(m, col0, width, on_vector=False):
             res = outp.tile([P, width], F32, name="res%d" % width)
@@ -202,69 +200,70 @@ def tile_mnelayer_pb_kernel(tc, potential, contribution, out):
         regroup_a(0, LEFT)
         nc.vector.tensor_copy(out=c_32[:], in_=c_bf[:])
         nc.vector.tensor_scalar(out=c_neg[:], in0=c_bf[:], scalar1=SLOPE, scalar2=None, op0=ALU.mult)
-        scale(0, LEFT)
         branches(0)
+        scale(0, LEFT)
         leak(1, LEFT)
         regroup_a(1, LEFT)
         collect(0)
         branches(1)
         scale(1, LEFT)
-        collect(1)
+        branches(2)
         leak(2, LEFT)
         regroup_a(2, LEFT)
+        collect(1)
         quantise_a(0, LEFT)
         quantise_w(0, RIGHT)
-        quantise_w(0, LEFT)
-        multiply_left(EARLY_TILES, 0)
-        leak(3, LEFT)
-        regroup_a(3, LEFT)
-        branches(2)
         scale(2, LEFT)
         collect(2)
+        leak(3, LEFT)
+        regroup_a(3, LEFT)
+        quantise_w(0, LEFT)
+        multiply_tiles(TILES, (0,), 0, HALF)
         quantise_a(1, LEFT)
         quantise_w(1, RIGHT)
         quantise_w(1, LEFT)
-        multiply_left(EARLY_TILES, 1)
+        multiply_tiles(TILES, (1,), 0, HALF)
         scale(3, LEFT)
-        multiply_left(LATE_TILES, 0)
-        multiply_left(LATE_TILES, 1)
         leak(LAST, RIGHT)
         quantise_a(2, LEFT)
         quantise_w(2, RIGHT)
-        multiply_left(RIGHT_TILES, 2)
+        multiply_tiles(RIGHT_TILES, (2,), 0, HALF)
         scale(LAST, RIGHT)
-        regroup_a(LAST, RIGHT)
         quantise_w(2, LEFT)
-        multiply_left(LEFT_TILES, 2)
+        multiply_tiles(LEFT_TILES, (2,), 0, HALF)
         quantise_a(3, LEFT)
         quantise_w(3, LEFT)
-        multiply_left(LEFT_TILES, 3)
+        multiply_tiles(LEFT_TILES, (3,), 0, HALF)
+        for m in LEFT_TILES:
+            finish(m, 0, HALF)
+        regroup_a(LAST, RIGHT)
         direct_a(0, 0)
         quantise_w(3, RIGHT)
-        multiply_left(RIGHT_TILES, 3)
-        for m in TILES:
+        multiply_tiles(RIGHT_TILES, (3,), 0, HALF)
+        for m in RIGHT_TILES:
             finish(m, 0, HALF)
 
         direct_a(1, 0)
         quantise_direct(0, 0)
+        multiply_tiles(LEFT_TILES, (0,), HALF, QUART)
         direct_a(2, 0)
         quantise_direct(1, 0)
-        quantise_a(LAST, RIGHT)
+        multiply_tiles(LEFT_TILES, (1,), HALF, QUART)
         quantise_direct(2, 0)
-        for m in TILES:
-            for c in range(PASSES):
-                multiply(m, c, HALF, QUART)
-
+        multiply_tiles(LEFT_TILES, (2,), HALF, QUART)
+        quantise_a(LAST, RIGHT)
         direct_a(0, 1)
+        multiply_tiles(LEFT_TILES, (3,), HALF, QUART)
         direct_a(1, 1)
         quantise_direct(0, 1)
+        multiply_by_tile(RIGHT_TILES, (0, 1, 2, 3), HALF, QUART)
+        for m in TILES:
+            finish(m, HALF, QUART)
+
         direct_a(2, 1)
         quantise_direct(1, 1)
         quantise_direct(2, 1)
-        for m in TILES:
-            finish(m, HALF, QUART)
-        for m in TILES:
-            for c in range(PASSES):
-                multiply(m, c, HALF + QUART, QUART)
+        multiply_tiles(LEFT_TILES, (3, 0, 1, 2), HALF + QUART, QUART)
+        multiply_by_tile(RIGHT_TILES, (3, 0, 1, 2), HALF + QUART, QUART)
         for i, m in enumerate(TILES):
-            finish(m, HALF + QUART, QUART, i % 2 == 0)
+            finish(m, HALF + QUART, QUART, i % 2 == 1)

@@ -39,6 +39,7 @@ def tile_mnelayer_pb_kernel(tc, potential, contribution, out):
         work = ctx.enter_context(tc.tile_pool(name="work", bufs=3))
         groups = ctx.enter_context(tc.tile_pool(name="groups", bufs=5))
         outp = ctx.enter_context(tc.tile_pool(name="outp", bufs=8))
+        outq = ctx.enter_context(tc.tile_pool(name="outq", bufs=16))
         psum = ctx.enter_context(tc.psum_pool(name="psum", bufs=8))
         ctx.enter_context(tc.manual_schedule())
 
@@ -85,7 +86,7 @@ def tile_mnelayer_pb_kernel(tc, potential, contribution, out):
             nc.vector.quantize_mx(
                 out=codes[:, c, cols].bitcast(FP8X4),
                 scales=scales[:, c, cols],
-                in_=grp[:].rearrange("p w j -> p (w j)"),
+                in_=grp.rearrange("p w j -> p (w j)"),
             )
 
         a_grp = {}
@@ -103,14 +104,15 @@ def tile_mnelayer_pb_kernel(tc, potential, contribution, out):
             else:
                 leaky_relu(leaky[(c, h)][:], right_half(c))
 
-        def regroup_a(c, h):
-            a_grp[(c, h)] = groups.tile([P, HALF, PACK], BF16, name="a_grp", align_bytes=64)
-            for col0, width in HEAD_PIECES if (c, h) == (0, LEFT) else ((0, HALF),):
+        def regroup_a(c, h, pieces=((0, HALF),)):
+            if (c, h) not in a_grp:
+                a_grp[(c, h)] = groups.tile([P, HALF, PACK], BF16, name="a_grp", align_bytes=64)
+            for col0, width in pieces:
                 cols = slice(col0, col0 + width)
                 nc.scalar.copy(out=grouped(a_grp[(c, h)][:, cols, :]), in_=rows_of(leaky[(c, h)][:, :, cols]))
 
-        def quantise_a(c, h):
-            quantise(a_grp[(c, h)], a_codes, a_scales, c, HALF * h, HALF)
+        def quantise_a(c, h, col0=0, width=HALF):
+            quantise(a_grp[(c, h)][:, col0 : col0 + width, :], a_codes, a_scales, c, HALF * h + col0, width)
 
         def direct_a(c, q):
             a_grp[(c, "q", q)] = groups.tile([P, QUART, PACK], BF16, name="d_grp", align_bytes=64)
@@ -118,7 +120,7 @@ def tile_mnelayer_pb_kernel(tc, potential, contribution, out):
             leaky_relu(a_grp[(c, "q", q)][:], x.rearrange("p j w -> p w j"))
 
         def quantise_direct(c, q):
-            quantise(a_grp[(c, "q", q)], a_codes, a_scales, c, HALF + QUART * q, QUART)
+            quantise(a_grp[(c, "q", q)][:], a_codes, a_scales, c, HALF + QUART * q, QUART)
 
         def scale(c, h):
             weighted = work.tile([P, PACK, HALF], BF16, name="weighted")
@@ -160,7 +162,7 @@ def tile_mnelayer_pb_kernel(tc, potential, contribution, out):
                 )
 
         def quantise_w(c, h):
-            quantise(w_grp[(c, h)], w_codes, w_scales, c, HALF * h, HALF)
+            quantise(w_grp[(c, h)][:], w_codes, w_scales, c, HALF * h, HALF)
 
         def multiply(m, c, col0, width):
             if (m, col0) not in acc:
@@ -188,7 +190,7 @@ def tile_mnelayer_pb_kernel(tc, potential, contribution, out):
                 multiply_tiles((m,), passes, col0, width)
 
         def finish(m, col0, width, on_vector=False):
-            res = outp.tile([P, width], F32, name="res%d" % width)
+            res = (outp if width == HALF else outq).tile([P, width], F32, name="res%d" % width)
             src = acc[(m, col0)][:, 0:width]
             if on_vector:
                 nc.vector.tensor_scalar(out=res[:], in0=src, scalar1=1.0 / B, scalar2=None, op0=ALU.mult)
@@ -197,7 +199,7 @@ def tile_mnelayer_pb_kernel(tc, potential, contribution, out):
             nc.sync.dma_start(out=out[P * m : P * (m + 1), col0 : col0 + width], in_=res[:])
 
         leak(0, LEFT)
-        regroup_a(0, LEFT)
+        regroup_a(0, LEFT, HEAD_PIECES)
         nc.vector.tensor_copy(out=c_32[:], in_=c_bf[:])
         nc.vector.tensor_scalar(out=c_neg[:], in0=c_bf[:], scalar1=SLOPE, scalar2=None, op0=ALU.mult)
         branches(0)
@@ -234,14 +236,16 @@ def tile_mnelayer_pb_kernel(tc, potential, contribution, out):
         quantise_a(3, LEFT)
         quantise_w(3, LEFT)
         multiply_tiles(LEFT_TILES, (3,), 0, HALF)
-        for m in LEFT_TILES:
+        for m in LEFT_TILES[1:]:
             finish(m, 0, HALF)
-        regroup_a(LAST, RIGHT)
+        regroup_a(LAST, RIGHT, ((0, QUART),))
         direct_a(0, 0)
+        finish(LEFT_TILES[0], 0, HALF, on_vector=True)
         quantise_w(3, RIGHT)
         multiply_tiles(RIGHT_TILES, (3,), 0, HALF)
         for m in RIGHT_TILES:
             finish(m, 0, HALF)
+        regroup_a(LAST, RIGHT, ((QUART, QUART),))
 
         direct_a(1, 0)
         quantise_direct(0, 0)
@@ -251,11 +255,12 @@ def tile_mnelayer_pb_kernel(tc, potential, contribution, out):
         multiply_tiles(LEFT_TILES, (1,), HALF, QUART)
         quantise_direct(2, 0)
         multiply_tiles(LEFT_TILES, (2,), HALF, QUART)
-        quantise_a(LAST, RIGHT)
+        quantise_a(LAST, RIGHT, 0, QUART)
         direct_a(0, 1)
         multiply_tiles(LEFT_TILES, (3,), HALF, QUART)
         direct_a(1, 1)
         quantise_direct(0, 1)
+        quantise_a(LAST, RIGHT, QUART, QUART)
         multiply_by_tile(RIGHT_TILES, (0, 1, 2, 3), HALF, QUART)
         for m in TILES:
             finish(m, HALF, QUART)

@@ -122,14 +122,17 @@ def tile_mnelayer_pb_kernel(tc, potential, contribution, out):
         def quantise_direct(c, q):
             quantise(a_grp[(c, "q", q)][:], a_codes, a_scales, c, HALF + QUART * q, QUART)
 
-        def scale(c, h):
+        def scale(c, h, on_scalar=False):
             weighted = work.tile([P, PACK, HALF], BF16, name="weighted")
             for j in range(PACK):
                 r = PACK * c + j
-                nc.vector.tensor_scalar(
-                    out=weighted[:, j, :], in0=leaky[(c, h)][:, j, :],
-                    scalar1=c_32[:, r : r + 1], scalar2=None, op0=ALU.mult,
-                )
+                if on_scalar:
+                    nc.scalar.activation(out=weighted[:, j, :], in_=leaky[(c, h)][:, j, :], func=ACT.Copy, scale=c_32[:, r : r + 1])
+                else:
+                    nc.vector.tensor_scalar(
+                        out=weighted[:, j, :], in0=leaky[(c, h)][:, j, :],
+                        scalar1=c_32[:, r : r + 1], scalar2=None, op0=ALU.mult,
+                    )
             w_grp[(c, h)] = groups.tile([P, HALF, PACK], BF16, name="w_grp", align_bytes=64)
             nc.scalar.copy(out=grouped(w_grp[(c, h)][:], 8), in_=rows_of(weighted[:], 8))
 
@@ -203,7 +206,7 @@ def tile_mnelayer_pb_kernel(tc, potential, contribution, out):
         nc.vector.tensor_copy(out=c_32[:], in_=c_bf[:])
         nc.vector.tensor_scalar(out=c_neg[:], in0=c_bf[:], scalar1=SLOPE, scalar2=None, op0=ALU.mult)
         branches(0)
-        scale(0, LEFT)
+        scale(0, LEFT, on_scalar=True)
         leak(1, LEFT)
         regroup_a(1, LEFT)
         collect(0)
@@ -236,11 +239,10 @@ def tile_mnelayer_pb_kernel(tc, potential, contribution, out):
         quantise_a(3, LEFT)
         quantise_w(3, LEFT)
         multiply_tiles(LEFT_TILES, (3,), 0, HALF)
-        for m in LEFT_TILES[1:]:
+        for m in LEFT_TILES:
             finish(m, 0, HALF)
         regroup_a(LAST, RIGHT, ((0, QUART),))
         direct_a(0, 0)
-        finish(LEFT_TILES[0], 0, HALF, on_vector=True)
         quantise_w(3, RIGHT)
         multiply_tiles(RIGHT_TILES, (3,), 0, HALF)
         for m in RIGHT_TILES:

@@ -122,11 +122,11 @@ def tile_mnelayer_pb_kernel(tc, potential, contribution, out):
         def quantise_direct(c, q):
             quantise(a_grp[(c, "q", q)][:], a_codes, a_scales, c, HALF + QUART * q, QUART)
 
-        def scale(c, h, on_scalar=False):
+        def scale(c, h, scalar_rows=0):
             weighted = work.tile([P, PACK, HALF], BF16, name="weighted")
             for j in range(PACK):
                 r = PACK * c + j
-                if on_scalar:
+                if j < scalar_rows:
                     nc.scalar.activation(out=weighted[:, j, :], in_=leaky[(c, h)][:, j, :], func=ACT.Copy, scale=c_32[:, r : r + 1])
                 else:
                     nc.vector.tensor_scalar(
@@ -206,7 +206,7 @@ def tile_mnelayer_pb_kernel(tc, potential, contribution, out):
         nc.vector.tensor_copy(out=c_32[:], in_=c_bf[:])
         nc.vector.tensor_scalar(out=c_neg[:], in0=c_bf[:], scalar1=SLOPE, scalar2=None, op0=ALU.mult)
         branches(0)
-        scale(0, LEFT, on_scalar=True)
+        scale(0, LEFT, scalar_rows=2)
         leak(1, LEFT)
         regroup_a(1, LEFT)
         collect(0)

@@ -109,7 +109,7 @@ def tile_mnelayer_pb_kernel(tc, potential, contribution, out):
                 a_grp[(c, h)] = groups.tile([P, HALF, PACK], BF16, name="a_grp", align_bytes=64)
             for col0, width in pieces:
                 cols = slice(col0, col0 + width)
-                nc.scalar.copy(out=grouped(a_grp[(c, h)][:, cols, :]), in_=rows_of(leaky[(c, h)][:, :, cols]))
+                nc.scalar.copy(out=grouped(a_grp[(c, h)][:, cols, :], 2), in_=rows_of(leaky[(c, h)][:, :, cols], 2))
 
         def quantise_a(c, h, col0=0, width=HALF):
             quantise(a_grp[(c, h)][:, col0 : col0 + width, :], a_codes, a_scales, c, HALF * h + col0, width)

@@ -109,7 +109,8 @@ def tile_mnelayer_pb_kernel(tc, potential, contribution, out):
                 a_grp[(c, h)] = groups.tile([P, HALF, PACK], BF16, name="a_grp", align_bytes=64)
             for col0, width in pieces:
                 cols = slice(col0, col0 + width)
-                nc.scalar.copy(out=grouped(a_grp[(c, h)][:, cols, :], 2), in_=rows_of(leaky[(c, h)][:, :, cols], 2))
+                run = 2 if width == HALF else 4
+                nc.scalar.copy(out=grouped(a_grp[(c, h)][:, cols, :], run), in_=rows_of(leaky[(c, h)][:, :, cols], run))
 
         def quantise_a(c, h, col0=0, width=HALF):
             quantise(a_grp[(c, h)][:, col0 : col0 + width, :], a_codes, a_scales, c, HALF * h + col0, width)
@@ -202,9 +203,10 @@ def tile_mnelayer_pb_kernel(tc, potential, contribution, out):
             nc.sync.dma_start(out=out[P * m : P * (m + 1), col0 : col0 + width], in_=res[:])
 
         leak(0, LEFT)
-        regroup_a(0, LEFT, HEAD_PIECES)
-        nc.vector.tensor_copy(out=c_32[:], in_=c_bf[:])
-        nc.vector.tensor_scalar(out=c_neg[:], in0=c_bf[:], scalar1=SLOPE, scalar2=None, op0=ALU.mult)
+        regroup_a(0, LEFT, HEAD_PIECES[:2])
+        nc.scalar.copy(out=c_32[:], in_=c_bf[:])
+        nc.scalar.activation(out=c_neg[:], in_=c_bf[:], func=ACT.Copy, scale=SLOPE)
+        regroup_a(0, LEFT, HEAD_PIECES[2:])
         branches(0)
         scale(0, LEFT, scalar_rows=2)
         leak(1, LEFT)

from contextlib import ExitStack

import concourse.mybir as mybir
from concourse.masks import make_identity

F32 = mybir.dt.float32
BF16 = mybir.dt.bfloat16
U32 = mybir.dt.uint32
U8 = mybir.dt.uint8
FP8X4 = mybir.dt.float8_e4m3fn_x4
ALU = mybir.AluOpType
ACT = mybir.ActivationFunctionType

P = 128
B = 2048
N = 1024
PACK = 4
PASSES = B // (P * PACK)
ROWS = PASSES * PACK
HALF = 512
QUART = 256
SLOPE = 0.01
FLOPS = 2 * B * N * N

LAST = PASSES - 1
LEFT, RIGHT = 0, 1
LEFT_TILES = (0, 1, 2, 3)
RIGHT_TILES = (4, 5, 6, 7)
HEAD_PIECES = ((0, 128), (128, 128), (256, 256))
TILES = LEFT_TILES + RIGHT_TILES


def tile_mnelayer_pb_kernel(tc, potential, contribution, out):
    nc = tc.nc
    pot = potential.rearrange("(c p j) w -> c p j w", c=PASSES, p=P, j=PACK)

    with ExitStack() as ctx:
        keep = ctx.enter_context(tc.tile_pool(name="keep", bufs=1))
        work = ctx.enter_context(tc.tile_pool(name="work", bufs=3))
        groups = ctx.enter_context(tc.tile_pool(name="groups", bufs=5))
        outp = ctx.enter_context(tc.tile_pool(name="outp", bufs=8))
        outq = ctx.enter_context(tc.tile_pool(name="outq", bufs=16))
        psum = ctx.enter_context(tc.psum_pool(name="psum", bufs=8))
        ctx.enter_context(tc.manual_schedule())

        c_bf = keep.tile([P, ROWS], BF16, name="c_bf")
        c_32 = keep.tile([P, ROWS], F32, name="c_32")
        c_neg = keep.tile([P, ROWS], F32, name="c_neg")
        ident = keep.tile([P, P], BF16, name="ident")
        first = [keep.tile([P, PACK, width], BF16, name="first%d" % col0) for col0, width in HEAD_PIECES]
        right0 = keep.tile([P, PACK, HALF], BF16, name="right0")
        p_in = [keep.tile([P, PACK, N], BF16, name="p_in%d" % c) for c in range(1, PASSES)]
        leaky = {}
        for c, h in ((0, LEFT), (1, LEFT), (2, LEFT), (3, LEFT), (LAST, RIGHT)):
            leaky[(c, h)] = keep.tile([P, PACK, HALF], F32, name="leaky%d%d" % (c, h))
        a_codes = keep.tile([P, PASSES, N], U32, name="a_codes", align_bytes=64)
        a_scales = keep.tile([P, PASSES, N], U8, name="a_scales", align_bytes=64)
        w_codes = keep.tile([P, PASSES, N], U32, name="w_codes", align_bytes=64)
        w_scales = keep.tile([P, PASSES, N], U8, name="w_scales", align_bytes=64)

        nc.scalar.dma_start(
            out=c_bf[:].rearrange("p (c j) -> p c j", j=PACK),
            in_=contribution.rearrange("(c p j) -> p c j", c=PASSES, p=P),
        )
        for (col0, width), piece in zip(HEAD_PIECES, first):
            nc.sync.dma_start(out=piece[:], in_=pot[0][:, :, col0 : col0 + width])
        nc.sync.dma_start(out=right0[:], in_=pot[0][:, :, HALF:N])
        for c in range(1, PASSES):
            nc.sync.dma_start(out=p_in[c - 1][:], in_=pot[c])
        make_identity(nc, ident[:])

        def right_half(c):
            return right0[:] if c == 0 else p_in[c - 1][:, :, HALF:N]

        def grouped(dst, run=4):
            return dst.rearrange("p (g i) j -> p g j i", i=run)

        def rows_of(src, run=4):
            return src.rearrange("p j (g i) -> p g j i", i=run)

        def leaky_relu(dst, src):
            nc.vector.scalar_tensor_tensor(out=dst, in0=src, scalar=SLOPE, in1=src, op0=ALU.mult, op1=ALU.max)

        def quantise(grp, codes, scales, c, col0, width):
            cols = slice(col0, col0 + width)
            nc.vector.quantize_mx(
                out=codes[:, c, cols].bitcast(FP8X4),
                scales=scales[:, c, cols],
                in_=grp.rearrange("p w j -> p (w j)"),
            )

        a_grp = {}
        w_grp = {}
        banks = {}
        acc = {}
        done = {}

        def leak(c, h):
            if (c, h) == (0, LEFT):
                for (col0, width), piece in zip(HEAD_PIECES, first):
                    leaky_relu(leaky[(0, LEFT)][:, :, col0 : col0 + width], piece[:])
            elif h == LEFT:
                leaky_relu(leaky[(c, h)][:], p_in[c - 1][:, :, 0:HALF])
            else:
                leaky_relu(leaky[(c, h)][:], right_half(c))

        def regroup_a(c, h, pieces=((0, HALF),)):
            if (c, h) not in a_grp:
                a_grp[(c, h)] = groups.tile([P, HALF, PACK], BF16, name="a_grp", align_bytes=64)
            for col0, width in pieces:
                cols = slice(col0, col0 + width)
                run = 2 if width == HALF else 4
                nc.scalar.copy(out=grouped(a_grp[(c, h)][:, cols, :], run), in_=rows_of(leaky[(c, h)][:, :, cols], run))

        def quantise_a(c, h, col0=0, width=HALF):
            quantise(a_grp[(c, h)][:, col0 : col0 + width, :], a_codes, a_scales, c, HALF * h + col0, width)

        def direct_a(c, q):
            a_grp[(c, "q", q)] = groups.tile([P, QUART, PACK], BF16, name="d_grp", align_bytes=64)
            x = right_half(c)[:, :, QUART * q : QUART * (q + 1)]
            leaky_relu(a_grp[(c, "q", q)][:], x.rearrange("p j w -> p w j"))

        def quantise_direct(c, q):
            quantise(a_grp[(c, "q", q)][:], a_codes, a_scales, c, HALF + QUART * q, QUART)

        def scale(c, h, scalar_rows=0):
            weighted = work.tile([P, PACK, HALF], BF16, name="weighted")
            for j in range(PACK):
                r = PACK * c + j
                if j < scalar_rows:
                    nc.scalar.activation(out=weighted[:, j, :], in_=leaky[(c, h)][:, j, :], func=ACT.Copy, scale=c_32[:, r : r + 1])
                else:
                    nc.vector.tensor_scalar(
                        out=weighted[:, j, :], in0=leaky[(c, h)][:, j, :],
                        scalar1=c_32[:, r : r + 1], scalar2=None, op0=ALU.mult,
                    )
            w_grp[(c, h)] = groups.tile([P, HALF, PACK], BF16, name="w_grp", align_bytes=64)
            nc.scalar.copy(out=grouped(w_grp[(c, h)][:], 8), in_=rows_of(weighted[:], 8))

        def branches(c):
            pos = work.tile([P, PACK, HALF], BF16, name="pos")
            neg = work.tile([P, PACK, HALF], BF16, name="neg")
            x = right_half(c)
            for j in range(PACK):
                r = PACK * c + j
                nc.vector.tensor_scalar(
                    out=pos[:, j, :], in0=x[:, j, :], scalar1=0.0, scalar2=c_32[:, r : r + 1], op0=ALU.max, op1=ALU.mult,
                )
                nc.vector.tensor_scalar(
                    out=neg[:, j, :], in0=x[:, j, :], scalar1=0.0, scalar2=c_neg[:, r : r + 1], op0=ALU.min, op1=ALU.mult,
                )
            w_grp[(c, RIGHT)] = groups.tile([P, HALF, PACK], BF16, name="w_grp", align_bytes=64)
            for q in range(2):
                bank = psum.tile([P, PACK * QUART], BF16, name="bank")
                for s in range(2):
                    cols = slice(QUART * q + P * s, QUART * q + P * (s + 1))
                    half_bank = grouped(bank[:, HALF * s : HALF * (s + 1)].rearrange("p (w j) -> p w j", j=PACK), 8)
                    nc.tensor.matmul(out=half_bank, lhsT=ident[:], rhs=rows_of(pos[:, :, cols], 8), start=True, stop=False)
                    nc.tensor.matmul(out=half_bank, lhsT=ident[:], rhs=rows_of(neg[:, :, cols], 8), start=False, stop=True)
                banks[(c, q)] = bank

        def collect(c):
            for q in range(2):
                nc.scalar.copy(
                    out=w_grp[(c, RIGHT)][:, QUART * q : QUART * (q + 1), :].rearrange("p w j -> p (w j)"), in_=banks[(c, q)][:],
                )

        def quantise_w(c, h):
            quantise(w_grp[(c, h)][:], w_codes, w_scales, c, HALF * h, HALF)

        def multiply(m, c, col0, width):
            if (m, col0) not in acc:
                acc[(m, col0)] = psum.tile([P, HALF], F32, name="bank")
            done[(m, col0)] = done.get((m, col0), 0) + 1
            lcols = slice(P * m, P * (m + 1))
            rcols = slice(col0, col0 + width)
            nc.tensor.matmul_mx(
                out=acc[(m, col0)][:, 0:width],
                lhsT=w_codes[:, c, lcols].bitcast(FP8X4),
                lhsT_scale=w_scales[:, c, lcols],
                rhs=a_codes[:, c, rcols].bitcast(FP8X4),
                rhs_scale=a_scales[:, c, rcols],
                start=done[(m, col0)] == 1,
                stop=done[(m, col0)] == PASSES,
            )

        def multiply_tiles(tiles, passes, col0, width):
            for c in passes:
                for m in tiles:
                    multiply(m, c, col0, width)

        def multiply_by_tile(tiles, passes, col0, width):
            for m in tiles:
                multiply_tiles((m,), passes, col0, width)

        def finish(m, col0, width, on_vector=False):
            res = (outp if width == HALF else outq).tile([P, width], F32, name="res%d" % width)
            src = acc[(m, col0)][:, 0:width]
            if on_vector:
                nc.vector.tensor_scalar(out=res[:], in0=src, scalar1=1.0 / B, scalar2=None, op0=ALU.mult)
            else:
                nc.scalar.activation(out=res[:], in_=src, func=ACT.Copy, scale=1.0 / B)
            nc.sync.dma_start(out=out[P * m : P * (m + 1), col0 : col0 + width], in_=res[:])

        leak(0, LEFT)
        regroup_a(0, LEFT, HEAD_PIECES[:2])
        nc.scalar.copy(out=c_32[:], in_=c_bf[:])
        nc.scalar.activation(out=c_neg[:], in_=c_bf[:], func=ACT.Copy, scale=SLOPE)
        regroup_a(0, LEFT, HEAD_PIECES[2:])
        branches(0)
        scale(0, LEFT, scalar_rows=2)
        leak(1, LEFT)
        regroup_a(1, LEFT)
        collect(0)
        branches(1)
        scale(1, LEFT)
        branches(2)
        leak(2, LEFT)
        regroup_a(2, LEFT)
        collect(1)
        quantise_a(0, LEFT)
        quantise_w(0, RIGHT)
        scale(2, LEFT)
        collect(2)
        leak(3, LEFT)
        regroup_a(3, LEFT)
        quantise_w(0, LEFT)
        multiply_tiles(TILES, (0,), 0, HALF)
        quantise_a(1, LEFT)
        quantise_w(1, RIGHT)
        quantise_w(1, LEFT)
        multiply_tiles(TILES, (1,), 0, HALF)
        scale(3, LEFT)
        leak(LAST, RIGHT)
        quantise_a(2, LEFT)
        quantise_w(2, RIGHT)
        multiply_tiles(RIGHT_TILES, (2,), 0, HALF)
        scale(LAST, RIGHT)
        quantise_w(2, LEFT)
        multiply_tiles(LEFT_TILES, (2,), 0, HALF)
        quantise_a(3, LEFT)
        quantise_w(3, LEFT)
        multiply_tiles(LEFT_TILES, (3,), 0, HALF)
        for m in LEFT_TILES:
            finish(m, 0, HALF)
        regroup_a(LAST, RIGHT, ((0, QUART),))
        direct_a(0, 0)
        quantise_w(3, RIGHT)
        multiply_tiles(RIGHT_TILES, (3,), 0, HALF)
        for m in RIGHT_TILES:
            finish(m, 0, HALF)
        regroup_a(LAST, RIGHT, ((QUART, QUART),))

        direct_a(1, 0)
        quantise_direct(0, 0)
        multiply_tiles(LEFT_TILES, (0,), HALF, QUART)
        direct_a(2, 0)
        quantise_direct(1, 0)
        multiply_tiles(LEFT_TILES, (1,), HALF, QUART)
        quantise_direct(2, 0)
        multiply_tiles(LEFT_TILES, (2,), HALF, QUART)
        quantise_a(LAST, RIGHT, 0, QUART)
        direct_a(0, 1)
        multiply_tiles(LEFT_TILES, (3,), HALF, QUART)
        direct_a(1, 1)
        quantise_direct(0, 1)
        quantise_a(LAST, RIGHT, QUART, QUART)
        multiply_by_tile(RIGHT_TILES, (0, 1, 2, 3), HALF, QUART)
        for m in TILES:
            finish(m, HALF, QUART)

        direct_a(2, 1)
        quantise_direct(1, 1)
        quantise_direct(2, 1)
        multiply_tiles(LEFT_TILES, (3, 0, 1, 2), HALF + QUART, QUART)
        multiply_by_tile(RIGHT_TILES, (3, 0, 1, 2), HALF + QUART, QUART)
        for i, m in enumerate(TILES):
            finish(m, HALF + QUART, QUART, i % 2 == 1)
